import numpy as np
import ml_dtypes


def mxq(x, axis, fmt="e4m3"):
    dtype, down = {"e4m3": (ml_dtypes.float8_e4m3fn, 7), "e5m2": (ml_dtypes.float8_e5m2, 14)}[fmt]
    v = np.moveaxis(np.asarray(x, np.float32).astype(ml_dtypes.bfloat16).astype(np.float64), axis, -1)
    blocks = v.reshape(v.shape[:-1] + (-1, 32))
    amax = np.abs(blocks).max(-1, keepdims=True)
    byte = np.maximum(np.where(amax > 0, np.frexp(amax)[1] - 1 + 127, 0) - down, 1)
    scale = np.exp2(byte - 127.0)
    codes = (blocks / scale).astype(np.float32).astype(dtype).astype(np.float64)
    return np.moveaxis((codes * scale).reshape(v.shape), -1, axis)


WIDE = False


def mx_kscale(k):
    if not WIDE:
        return np.ones(k)
    levels = np.array([20, -20, 10, -10, 0])
    a = np.random.permutation(np.resize(levels, k // 512 * 4)).reshape(k // 512, 4)
    idx = np.arange(k)
    return np.exp2(a[idx // 512, idx % 128 // 32])


BF16 = ml_dtypes.bfloat16


def bf(x):
    return np.asarray(x, np.float32).astype(BF16)


def f64(x):
    return np.asarray(x).astype(np.float64)


B, N, D = 4, 2, 512


def select_func(A1):
    return np.mean(np.abs(A1), axis=(-2, -1), keepdims=True) > 1.0


def reset_func(A1):
    return A1 / np.max(np.abs(A1), axis=(-2, -1), keepdims=True)


def setup_inputs():
    s = mx_kscale(N * D).reshape(N, 1, D)
    kind = np.random.permutation(np.arange(B) % 4).reshape(B, 1, 1, 1)
    large = kind < 2
    zero_bias = kind % 2 == 0
    scale = np.where(large, np.random.uniform(2.2, 3.0, (B, 1, 1, 1)), np.random.uniform(0.3, 0.6, (B, 1, 1, 1)))
    A1 = np.random.standard_normal((B, 1, D, D)) * scale
    flat = A1.reshape(B, -1)
    peak = np.argmax(np.abs(flat), axis=1)
    flat[np.arange(B), peak] *= 1.25
    B1 = np.random.standard_normal((B, 1, D, D)) * 0.7 * np.where(zero_bias, 0.0, 1.0)
    A2 = np.random.standard_normal((B, N, D, D)) * 1.5 / np.sqrt(D) / s
    B2 = np.random.standard_normal((B, N, D, D))
    g = np.random.standard_normal((B, N, 2 * D, D)) * np.exp2(np.random.randint(-12, 1, (B, N, 1, D))) * 8.0 * s
    return {"A1_atop_B1": bf(np.concatenate([A1, B1], axis=-2)),
            "A2_atop_B2": bf(np.concatenate([A2, B2], axis=-2)),
            "grad_out": bf(g)}


def reference(A1_atop_B1, A2_atop_B2, grad_out):
    d = D
    left = f64(A1_atop_B1)
    A1 = left[..., :d, :]
    B1 = left[..., d:, :]
    A2 = f64(A2_atop_B2)[..., :d, :]
    g = f64(grad_out)
    gk = g.transpose(0, 2, 1, 3).reshape(B, 2 * d, N * d)
    ak = A2.transpose(0, 2, 1, 3).reshape(B, d, N * d)
    p = (mxq(gk, 2, "e5m2") @ mxq(ak, 2, "e4m3").transpose(0, 2, 1))[:, None]
    gA = p[..., :d, :]
    gB = p[..., d:, :]
    should_reset = select_func(A1) & np.all(B1 == 0, axis=(-2, -1), keepdims=True)
    m = np.max(np.abs(A1), axis=(-2, -1), keepdims=True)
    hit = np.where(np.abs(A1) == m, 1.0, 0.0)
    count = np.sum(hit, axis=(-2, -1), keepdims=True)
    dot = np.sum(gA * A1, axis=(-2, -1), keepdims=True)
    gA_reset = gA / m - np.sign(A1) * hit / count * dot / (m * m)
    return np.concatenate([np.where(should_reset, gA_reset, gA),
                           np.where(should_reset, np.zeros_like(gB), gB)], axis=-2)

@@ -1,0 +1,267 @@
+from contextlib import ExitStack
+
+import concourse.mybir as mybir
+from concourse.masks import make_identity
+
+F32 = mybir.dt.float32
+BF16 = mybir.dt.bfloat16
+U32 = mybir.dt.uint32
+U8 = mybir.dt.uint8
+E4 = mybir.dt.float8_e4m3fn_x4
+E5 = mybir.dt.float8_e5m2_x4
+ALU = mybir.AluOpType
+ACTF = mybir.ActivationFunctionType
+AX = mybir.AxisListType
+
+B = 4
+N = 2
+D = 512
+P = 128
+FLOPS = 2 * B * (2 * D) * D * (N * D)
+BYTES = B * (2 * D * D * 2 + N * D * D * 2 + N * 2 * D * D * 2 + 2 * D * D * 4)
+MANUAL = True
+
+
+def tile_updateonrightwithselectiveresetonleft_kernel(tc, A1_atop_B1, A2_atop_B2, grad_out, out):
+    nc = tc.nc
+    with ExitStack() as ctx:
+        const = ctx.enter_context(tc.tile_pool(name="const", bufs=1))
+        a1p = ctx.enter_context(tc.tile_pool(name="a1p", bufs=4))
+        b1p = ctx.enter_context(tc.tile_pool(name="b1p", bufs=4))
+        wtp = ctx.enter_context(tc.tile_pool(name="wtp", bufs=4))
+        a2p = ctx.enter_context(tc.tile_pool(name="a2p", bufs=6))
+        gp = ctx.enter_context(tc.tile_pool(name="gp", bufs=6))
+        grpp = ctx.enter_context(tc.tile_pool(name="grpp", bufs=4))
+        codep = ctx.enter_context(tc.tile_pool(name="codep", bufs=2))
+        op = ctx.enter_context(tc.tile_pool(name="op", bufs=4))
+        smallp = ctx.enter_context(tc.tile_pool(name="smallp", bufs=2))
+        xtp = ctx.enter_context(tc.psum_pool(name="xtp", bufs=3))
+        accp = ctx.enter_context(tc.psum_pool(name="accp", bufs=4))
+        statp = ctx.enter_context(tc.psum_pool(name="statp", bufs=1))
+        if MANUAL:
+            ctx.enter_context(tc.manual_schedule())
+
+        ident = const.tile([P, P], F32, name="ident")
+        make_identity(nc, ident[:])
+        ones = const.tile([P, P], F32, name="ones")
+        nc.vector.memset(ones[:], 1.0)
+        sa = const.tile([P, B], F32, name="sa")
+        mx = const.tile([P, B], F32, name="mx")
+        nz = const.tile([P, B], F32, name="nz")
+        sc = const.tile([P, 40], F32, name="sc")
+        junk = const.tile([P, 2 * D], F32, name="junk")
+        pst = statp.tile([P, D], F32, name="pst")
+        m4 = sc[:, 0:4]
+        z4 = sc[:, 4:8]
+        tz = sc[:, 8:12]
+        rs = sc[:, 12:16]
+        gm = sc[:, 16:20]
+        ms = sc[:, 20:24]
+        iv = sc[:, 24:28]
+        uu = sc[:, 28:32]
+        al = sc[:, 32:36]
+        kn = sc[:, 36:40]
+
+        a1 = {}
+        b1 = {}
+        wt = {}
+        a2 = {}
+        g = {}
+
+        def load_ab(b):
+            a1[b] = a1p.tile([P, 4 * D], BF16, name="a1")
+            nc.sync.dma_start(out=a1[b][:], in_=A1_atop_B1[b, 0, 0:D, :].rearrange("(p t) j -> p (t j)", p=P, t=4))
+            b1[b] = b1p.tile([P, 4 * D], BF16, name="b1")
+            nc.sync.dma_start(out=b1[b][:], in_=A1_atop_B1[b, 0, D:2 * D, :].rearrange("(p t) j -> p (t j)", p=P, t=4))
+
+        def load_mm(b):
+            for n in range(N):
+                a2[b, n] = a2p.tile([P, 4 * D], BF16, name="a2")
+                nc.sync.dma_start(
+                    out=a2[b, n][:].rearrange("p (h c) -> p h c", h=2),
+                    in_=A2_atop_B2[b, n, 0:D, :].rearrange("(h p t) j -> p h (t j)", h=2, p=P, t=2),
+                )
+            for n in range(N):
+                g[b, n] = gp.tile([P, 8 * D], BF16, name="g")
+                nc.sync.dma_start(
+                    out=g[b, n][:].rearrange("p (h c) -> p h c", h=2),
+                    in_=grad_out[b, n].rearrange("(h p t) j -> p h (t j)", h=2, p=P, t=4),
+                )
+
+        for b in range(B):
+            load_ab(b)
+        for b in range(3):
+            load_mm(b)
+
+        for b in range(B):
+            wt[b] = wtp.tile([P, 4 * D], BF16, name="wt")
+            nc.scalar.activation(out=wt[b][:], in_=a1[b][:], func=ACTF.Abs, accum_out=sa[:, b:b + 1])
+            nc.vector.tensor_scalar(out=b1[b][:], in0=b1[b][:], scalar1=0.0, scalar2=None, op0=ALU.not_equal,
+                                    op1=ALU.add, accum_out=nz[:, b:b + 1])
+            nc.vector.tensor_scalar(out=wt[b][:], in0=wt[b][:], scalar1=1.0, scalar2=None, op0=ALU.mult,
+                                    op1=ALU.max, accum_out=mx[:, b:b + 1])
+
+        def stat_chain():
+            pmx = accp.tile([P, D], F32, name="acc")
+            nc.tensor.matmul(out=pst[:, 0:4], lhsT=ones[:], rhs=sa[:], start=True, stop=True)
+            nc.tensor.matmul(out=pst[:, 4:8], lhsT=ones[:], rhs=nz[:], start=True, stop=True)
+            for b in range(B):
+                nc.tensor.matmul(out=pmx[:, b * P:(b + 1) * P], lhsT=mx[:, b:b + 1].to_broadcast([P, P]),
+                                 rhs=ident[:], start=True, stop=True)
+            nc.vector.tensor_reduce(out=m4, in_=pmx[:].rearrange("p (b c) -> p b c", b=B), axis=AX.X, op=ALU.max)
+            nc.vector.tensor_scalar(out=z4, in0=pst[:, 4:8], scalar1=0.0, scalar2=None, op0=ALU.is_equal)
+            nc.vector.tensor_tensor(out=tz, in0=z4, in1=pst[:, 0:4], op=ALU.mult)
+            nc.vector.tensor_scalar(out=rs, in0=tz, scalar1=float(D * D), scalar2=None, op0=ALU.is_gt)
+            nc.vector.tensor_scalar(out=gm, in0=tz, scalar1=float(D * D), scalar2=None, op0=ALU.is_le)
+            nc.vector.tensor_scalar(out=ms, in0=m4, scalar1=1.0, scalar2=None, op0=ALU.max)
+            nc.vector.reciprocal(out=iv, in_=ms)
+            nc.vector.tensor_tensor(out=uu, in0=rs, in1=iv, op=ALU.mult)
+            nc.vector.tensor_tensor(out=al, in0=uu, in1=gm, op=ALU.add)
+            nc.vector.scalar_tensor_tensor(out=kn, in0=uu, scalar=-1.0, in1=iv, op0=ALU.mult, op1=ALU.mult)
+
+        grp = {}
+        codes = {}
+        st = {}
+        osb = {}
+
+        def alloc_codes(b):
+            codes[b] = (
+                codep.tile([P, N * 2 * D], U32, name="gc", align_bytes=64),
+                codep.tile([P, N * 2 * D], U8, name="gs", align_bytes=64),
+                codep.tile([P, N * D], U32, name="ac", align_bytes=64),
+                codep.tile([P, N * D], U8, name="as_", align_bytes=64),
+            )
+
+        BANKS = [("a", 0, 0, 0), ("a", 0, 1, 0), ("a", 1, 0, 0), ("a", 1, 1, 0),
+                 ("g", 0, 0, 0), ("g", 0, 0, 1), ("g", 1, 0, 0), ("g", 1, 0, 1),
+                 ("g", 0, 1, 0), ("g", 0, 1, 1), ("g", 1, 1, 0), ("g", 1, 1, 1)]
+
+        def transpose_bank(b, i):
+            kind, n, h, pr = BANKS[i]
+            xt = xtp.tile([P, 4, P], F32, name="xt")
+            if kind == "a":
+                src = a2[b, n][:].bitcast(F32)
+                base = h * 512
+                key = (b, "a", n)
+                first = h == 0
+            else:
+                src = g[b, n][:].bitcast(F32)
+                base = h * 1024 + pr * 512
+                key = (b, "g", n, h)
+                first = pr == 0
+            for s in range(4):
+                nc.tensor.transpose(xt[:, s, :], src[:, base + s * P:base + (s + 1) * P], ident[:])
+            if first:
+                grp[key] = grpp.tile([P, 4 * D], BF16, name="grp", align_bytes=64)
+            words = grp[key][:].bitcast(F32)
+            if kind == "a":
+                nc.scalar.copy(out=words[:, h * 512:(h + 1) * 512].rearrange("q (r s) -> q r s", s=4),
+                               in_=xt[:].rearrange("q s r -> q r s"))
+            else:
+                nc.scalar.copy(out=words[:, pr * 512:(pr + 1) * 512].rearrange("q (t r u) -> q t r u", t=2, u=2),
+                               in_=xt[:].rearrange("q (t u) r -> q t r u", t=2, u=2))
+
+        def quantise(b, kind, n, h):
+            gc, gs, ac, as_ = codes[b]
+            if kind == "a":
+                cols = slice(n * D, (n + 1) * D)
+                nc.vector.quantize_mx(out=ac[:, cols].bitcast(E4), scales=as_[:, cols], in_=grp[b, "a", n][:])
+            else:
+                lo = n * 2 * D + h * D
+                cols = slice(lo, lo + D)
+                nc.vector.quantize_mx(out=gc[:, cols].bitcast(E5), scales=gs[:, cols], in_=grp[b, "g", n, h][:])
+
+        def mx_tile(b, ti):
+            gc, gs, ac, as_ = codes[b]
+            h = ti // 4
+            t = ti % 4
+            if t == 0:
+                osb[b, h] = op.tile([P, 4 * D], F32, name="osb")
+            acc = accp.tile([P, D], F32, name="acc")
+            for n in range(N):
+                lo = n * 2 * D + ti * P
+                nc.tensor.matmul_mx(out=acc[:], lhsT=gc[:, lo:lo + P].bitcast(E5), lhsT_scale=gs[:, lo:lo + P],
+                                    rhs=ac[:, n * D:(n + 1) * D].bitcast(E4), rhs_scale=as_[:, n * D:(n + 1) * D],
+                                    start=(n == 0), stop=(n == N - 1))
+            scale = al[:, b:b + 1] if h == 0 else gm[:, b:b + 1]
+            if ti >= 6 and b < B - 1:
+                nc.vector.tensor_scalar(out=osb[b, h][:, t * D:(t + 1) * D], in0=acc[:], scalar1=scale, scalar2=None,
+                                        op0=ALU.mult)
+            else:
+                nc.scalar.activation(out=osb[b, h][:, t * D:(t + 1) * D], in_=acc[:], func=ACTF.Copy, scale=scale)
+
+        def hits(b):
+            st[b] = smallp.tile([P, 4], F32, name="st")
+            for hf in range(2):
+                cols = slice(hf * 2 * D, (hf + 1) * 2 * D)
+                nc.vector.tensor_scalar(out=wt[b][:, cols], in0=wt[b][:, cols], scalar1=m4[:, b:b + 1], scalar2=None,
+                                        op0=ALU.is_equal, op1=ALU.add, accum_out=st[b][:, 2 + hf:3 + hf])
+            nc.vector.tensor_tensor(out=wt[b][:], in0=wt[b][:], in1=a1[b][:], op=ALU.mult)
+
+        def dot_half(b, hf):
+            cols = slice(hf * 2 * D, (hf + 1) * 2 * D)
+            nc.vector.scalar_tensor_tensor(out=junk[:], in0=osb[b, 0][:, cols], scalar=1.0, in1=a1[b][:, cols],
+                                           op0=ALU.mult, op1=ALU.mult, accum_out=st[b][:, hf:hf + 1])
+
+        def dot_sum(b):
+            nc.tensor.matmul(out=pst[:, 8 + 4 * b:12 + 4 * b], lhsT=ones[:], rhs=st[b][:], start=True, stop=True)
+
+        def store(b, h, lo, hi):
+            nc.sync.dma_start(out=out[b, 0, h * D:(h + 1) * D, :].rearrange("(p t) k -> p (t k)", p=P, t=4)[:, lo:hi],
+                              in_=osb[b, h][:, lo:hi])
+
+        def correct(b):
+            red = smallp.tile([P, 4], F32, name="red")
+            nc.vector.tensor_reduce(out=red[:, 0:2], in_=pst[:, 8 + 4 * b:12 + 4 * b].rearrange("p (a c) -> p a c", a=2),
+                                    axis=AX.X, op=ALU.add)
+            nc.vector.reciprocal(out=red[:, 2:3], in_=red[:, 1:2])
+            nc.vector.scalar_tensor_tensor(out=red[:, 3:4], in0=red[:, 0:1], scalar=kn[:, b:b + 1], in1=red[:, 2:3],
+                                           op0=ALU.mult, op1=ALU.mult)
+            pieces = 2 if b == B - 1 else 1
+            w = 4 * D // pieces
+            for i in range(pieces):
+                nc.vector.scalar_tensor_tensor(out=osb[b, 0][:, i * w:(i + 1) * w], in0=wt[b][:, i * w:(i + 1) * w],
+                                               scalar=red[:, 3:4], in1=osb[b, 0][:, i * w:(i + 1) * w],
+                                               op0=ALU.mult, op1=ALU.add)
+                store(b, 0, i * w, (i + 1) * w)
+
+        for r in range(B + 1):
+            tb = r
+            mb = r - 1
+            if tb < B:
+                alloc_codes(tb)
+            for s in range(4):
+                if s == 0 and mb >= 0:
+                    quantise(mb, "g", 0, 1)
+                    quantise(mb, "g", 1, 1)
+                if mb >= 0:
+                    mx_tile(mb, 2 * s)
+                    mx_tile(mb, 2 * s + 1)
+                    if s == 3:
+                        dot_sum(mb)
+                    if s == 2 and mb == B - 1:
+                        store(mb, 1, 0, 2 * D)
+                if tb < B:
+                    for i in range(3 * s, 3 * s + 3):
+                        transpose_bank(tb, i)
+                if mb >= 0 and s == 1:
+                    dot_half(mb, 0)
+                if mb >= 0 and s == 2:
+                    dot_half(mb, 1)
+                if tb < B:
+                    if s == 0:
+                        quantise(tb, "a", 0, 0)
+                    if s == 1:
+                        quantise(tb, "a", 1, 0)
+                        quantise(tb, "g", 0, 0)
+                    if s == 2:
+                        quantise(tb, "g", 1, 0)
+                if r == 0 and s == 1:
+                    stat_chain()
+                if mb >= 0 and s == 3:
+                    store(mb, 1, 2 * D if mb == B - 1 else 0, 4 * D)
+                    correct(mb)
+                if tb < B and s == 3:
+                    hits(tb)
+            if r == 0:
+                load_mm(3)

@@ -19,7 +19,7 @@ D = 512
 P = 128
 FLOPS = 2 * B * (2 * D) * D * (N * D)
 BYTES = B * (2 * D * D * 2 + N * D * D * 2 + N * 2 * D * D * 2 + 2 * D * D * 4)
-MANUAL = True
+MANUAL = False
 
 
 def tile_updateonrightwithselectiveresetonleft_kernel(tc, A1_atop_B1, A2_atop_B2, grad_out, out):

@@ -5,6 +5,7 @@ from concourse.masks import make_identity
 
 F32 = mybir.dt.float32
 BF16 = mybir.dt.bfloat16
+I32 = mybir.dt.int32
 U32 = mybir.dt.uint32
 U8 = mybir.dt.uint8
 E4 = mybir.dt.float8_e4m3fn_x4
@@ -27,14 +28,14 @@ def tile_updateonrightwithselectiveresetonleft_kernel(tc, A1_atop_B1, A2_atop_B2
     with ExitStack() as ctx:
         const = ctx.enter_context(tc.tile_pool(name="const", bufs=1))
         a1p = ctx.enter_context(tc.tile_pool(name="a1p", bufs=4))
-        b1p = ctx.enter_context(tc.tile_pool(name="b1p", bufs=4))
-        wtp = ctx.enter_context(tc.tile_pool(name="wtp", bufs=4))
+        b1p = ctx.enter_context(tc.tile_pool(name="b1p", bufs=3))
+        wtp = ctx.enter_context(tc.tile_pool(name="wtp", bufs=3))
         a2p = ctx.enter_context(tc.tile_pool(name="a2p", bufs=6))
         gp = ctx.enter_context(tc.tile_pool(name="gp", bufs=6))
         grpp = ctx.enter_context(tc.tile_pool(name="grpp", bufs=4))
         codep = ctx.enter_context(tc.tile_pool(name="codep", bufs=2))
         op = ctx.enter_context(tc.tile_pool(name="op", bufs=4))
-        smallp = ctx.enter_context(tc.tile_pool(name="smallp", bufs=2))
+        smallp = ctx.enter_context(tc.tile_pool(name="smallp", bufs=3))
         xtp = ctx.enter_context(tc.psum_pool(name="xtp", bufs=3))
         accp = ctx.enter_context(tc.psum_pool(name="accp", bufs=4))
         statp = ctx.enter_context(tc.psum_pool(name="statp", bufs=1))
@@ -45,36 +46,31 @@ def tile_updateonrightwithselectiveresetonleft_kernel(tc, A1_atop_B1, A2_atop_B2
         make_identity(nc, ident[:])
         ones = const.tile([P, P], F32, name="ones")
         nc.vector.memset(ones[:], 1.0)
-        sa = const.tile([P, B], F32, name="sa")
-        mx = const.tile([P, B], F32, name="mx")
-        nz = const.tile([P, B], F32, name="nz")
-        sc = const.tile([P, 40], F32, name="sc")
+        onesb = const.tile([P, P], BF16, name="onesb")
+        nc.vector.memset(onesb[:], 1.0)
         junk = const.tile([P, 2 * D], F32, name="junk")
+        junkb = const.tile([P, 4 * D], BF16, name="junkb")
+        junka = const.tile([P, D], BF16, name="junka")
         pst = statp.tile([P, D], F32, name="pst")
-        m4 = sc[:, 0:4]
-        z4 = sc[:, 4:8]
-        tz = sc[:, 8:12]
-        rs = sc[:, 12:16]
-        gm = sc[:, 16:20]
-        ms = sc[:, 20:24]
-        iv = sc[:, 24:28]
-        uu = sc[:, 28:32]
-        al = sc[:, 32:36]
-        kn = sc[:, 36:40]
 
         a1 = {}
         b1 = {}
         wt = {}
         a2 = {}
         g = {}
+        loc = {}
+        tot = {}
+        sc = {}
+        grp = {}
+        codes = {}
+        st = {}
+        osb = {}
 
-        def load_ab(b):
+        def load(b):
             a1[b] = a1p.tile([P, 4 * D], BF16, name="a1")
             nc.sync.dma_start(out=a1[b][:], in_=A1_atop_B1[b, 0, 0:D, :].rearrange("(p t) j -> p (t j)", p=P, t=4))
             b1[b] = b1p.tile([P, 4 * D], BF16, name="b1")
             nc.sync.dma_start(out=b1[b][:], in_=A1_atop_B1[b, 0, D:2 * D, :].rearrange("(p t) j -> p (t j)", p=P, t=4))
-
-        def load_mm(b):
             for n in range(N):
                 a2[b, n] = a2p.tile([P, 4 * D], BF16, name="a2")
                 nc.sync.dma_start(
@@ -88,41 +84,41 @@ def tile_updateonrightwithselectiveresetonleft_kernel(tc, A1_atop_B1, A2_atop_B2
                     in_=grad_out[b, n].rearrange("(h p t) j -> p h (t j)", h=2, p=P, t=4),
                 )
 
-        for b in range(B):
-            load_ab(b)
-        for b in range(3):
-            load_mm(b)
-
-        for b in range(B):
+        def stats_vector(b):
             wt[b] = wtp.tile([P, 4 * D], BF16, name="wt")
-            nc.scalar.activation(out=wt[b][:], in_=a1[b][:], func=ACTF.Abs, accum_out=sa[:, b:b + 1])
-            nc.vector.tensor_scalar(out=b1[b][:], in0=b1[b][:], scalar1=0.0, scalar2=None, op0=ALU.not_equal,
-                                    op1=ALU.add, accum_out=nz[:, b:b + 1])
-            nc.vector.tensor_scalar(out=wt[b][:], in0=wt[b][:], scalar1=1.0, scalar2=None, op0=ALU.mult,
-                                    op1=ALU.max, accum_out=mx[:, b:b + 1])
+            loc[b] = smallp.tile([P, 2], F32, name="loc")
+            nc.vector.tensor_scalar(out=wt[b][:].bitcast(I32), in0=a1[b][:].bitcast(I32), scalar1=0x7FFF7FFF,
+                                    scalar2=None, op0=ALU.bitwise_and)
+            nc.vector.tensor_scalar(out=junkb[:], in0=wt[b][:], scalar1=1.0, scalar2=None, op0=ALU.mult,
+                                    op1=ALU.max, accum_out=loc[b][:, 0:1])
+            nc.vector.tensor_scalar(out=junkb[:], in0=b1[b][:], scalar1=0.0, scalar2=None, op0=ALU.not_equal,
+                                    op1=ALU.max, accum_out=loc[b][:, 1:2])
 
-        def stat_chain():
-            pmx = accp.tile([P, D], F32, name="acc")
-            nc.tensor.matmul(out=pst[:, 0:4], lhsT=ones[:], rhs=sa[:], start=True, stop=True)
-            nc.tensor.matmul(out=pst[:, 4:8], lhsT=ones[:], rhs=nz[:], start=True, stop=True)
-            for b in range(B):
-                nc.tensor.matmul(out=pmx[:, b * P:(b + 1) * P], lhsT=mx[:, b:b + 1].to_broadcast([P, P]),
+        def stats_tensor(b):
+            ptot = accp.tile([P, D], F32, name="acc")
+            for t in range(4):
+                nc.tensor.matmul(out=ptot[:], lhsT=onesb[:], rhs=wt[b][:, t * D:(t + 1) * D], start=(t == 0), stop=(t == 3))
+            tot[b] = smallp.tile([P, 1], F32, name="tot")
+            nc.scalar.activation(out=junka[:], in_=ptot[:], func=ACTF.Copy, accum_out=tot[b][:])
+            for i in range(2):
+                nc.tensor.matmul(out=pst[:, i * P:(i + 1) * P], lhsT=loc[b][:, i:i + 1].to_broadcast([P, P]),
                                  rhs=ident[:], start=True, stop=True)
-            nc.vector.tensor_reduce(out=m4, in_=pmx[:].rearrange("p (b c) -> p b c", b=B), axis=AX.X, op=ALU.max)
-            nc.vector.tensor_scalar(out=z4, in0=pst[:, 4:8], scalar1=0.0, scalar2=None, op0=ALU.is_equal)
-            nc.vector.tensor_tensor(out=tz, in0=z4, in1=pst[:, 0:4], op=ALU.mult)
-            nc.vector.tensor_scalar(out=rs, in0=tz, scalar1=float(D * D), scalar2=None, op0=ALU.is_gt)
-            nc.vector.tensor_scalar(out=gm, in0=tz, scalar1=float(D * D), scalar2=None, op0=ALU.is_le)
-            nc.vector.tensor_scalar(out=ms, in0=m4, scalar1=1.0, scalar2=None, op0=ALU.max)
-            nc.vector.reciprocal(out=iv, in_=ms)
-            nc.vector.tensor_tensor(out=uu, in0=rs, in1=iv, op=ALU.mult)
-            nc.vector.tensor_tensor(out=al, in0=uu, in1=gm, op=ALU.add)
-            nc.vector.scalar_tensor_tensor(out=kn, in0=uu, scalar=-1.0, in1=iv, op0=ALU.mult, op1=ALU.mult)
 
-        grp = {}
-        codes = {}
-        st = {}
-        osb = {}
+        def stats_chain(b):
+            s = smallp.tile([P, 10], F32, name="sc")
+            sc[b] = s
+            nc.vector.tensor_reduce(out=s[:, 0:2], in_=pst[:, 0:2 * P].rearrange("p (a c) -> p a c", a=2), axis=AX.X,
+                                    op=ALU.max)
+            nc.vector.tensor_scalar(out=s[:, 2:3], in0=s[:, 1:2], scalar1=0.0, scalar2=tot[b][:], op0=ALU.is_equal,
+                                    op1=ALU.mult)
+            nc.vector.tensor_scalar(out=s[:, 3:4], in0=s[:, 2:3], scalar1=float(D * D), scalar2=None, op0=ALU.is_le)
+            nc.vector.tensor_scalar(out=s[:, 4:5], in0=s[:, 0:1], scalar1=1.0, scalar2=None, op0=ALU.max)
+            nc.vector.reciprocal(out=s[:, 5:6], in_=s[:, 4:5])
+            nc.vector.tensor_scalar(out=s[:, 6:7], in0=s[:, 3:4], scalar1=0.0, scalar2=s[:, 5:6], op0=ALU.is_equal,
+                                    op1=ALU.mult)
+            nc.vector.tensor_tensor(out=s[:, 7:8], in0=s[:, 6:7], in1=s[:, 3:4], op=ALU.add)
+            nc.vector.scalar_tensor_tensor(out=s[:, 8:9], in0=s[:, 6:7], scalar=-1.0, in1=s[:, 5:6], op0=ALU.mult,
+                                           op1=ALU.mult)
 
         def alloc_codes(b):
             codes[b] = (
@@ -183,18 +179,14 @@ def tile_updateonrightwithselectiveresetonleft_kernel(tc, A1_atop_B1, A2_atop_B2
                 nc.tensor.matmul_mx(out=acc[:], lhsT=gc[:, lo:lo + P].bitcast(E5), lhsT_scale=gs[:, lo:lo + P],
                                     rhs=ac[:, n * D:(n + 1) * D].bitcast(E4), rhs_scale=as_[:, n * D:(n + 1) * D],
                                     start=(n == 0), stop=(n == N - 1))
-            scale = al[:, b:b + 1] if h == 0 else gm[:, b:b + 1]
-            if ti >= 6 and b < B - 1:
-                nc.vector.tensor_scalar(out=osb[b, h][:, t * D:(t + 1) * D], in0=acc[:], scalar1=scale, scalar2=None,
-                                        op0=ALU.mult)
-            else:
-                nc.scalar.activation(out=osb[b, h][:, t * D:(t + 1) * D], in_=acc[:], func=ACTF.Copy, scale=scale)
+            scale = sc[b][:, 7:8] if h == 0 else sc[b][:, 3:4]
+            nc.scalar.activation(out=osb[b, h][:, t * D:(t + 1) * D], in_=acc[:], func=ACTF.Copy, scale=scale)
 
         def hits(b):
             st[b] = smallp.tile([P, 4], F32, name="st")
             for hf in range(2):
                 cols = slice(hf * 2 * D, (hf + 1) * 2 * D)
-                nc.vector.tensor_scalar(out=wt[b][:, cols], in0=wt[b][:, cols], scalar1=m4[:, b:b + 1], scalar2=None,
+                nc.vector.tensor_scalar(out=wt[b][:, cols], in0=wt[b][:, cols], scalar1=sc[b][:, 0:1], scalar2=None,
                                         op0=ALU.is_equal, op1=ALU.add, accum_out=st[b][:, 2 + hf:3 + hf])
             nc.vector.tensor_tensor(out=wt[b][:], in0=wt[b][:], in1=a1[b][:], op=ALU.mult)
 
@@ -204,7 +196,7 @@ def tile_updateonrightwithselectiveresetonleft_kernel(tc, A1_atop_B1, A2_atop_B2
                                            op0=ALU.mult, op1=ALU.mult, accum_out=st[b][:, hf:hf + 1])
 
         def dot_sum(b):
-            nc.tensor.matmul(out=pst[:, 8 + 4 * b:12 + 4 * b], lhsT=ones[:], rhs=st[b][:], start=True, stop=True)
+            nc.tensor.matmul(out=pst[:, 256 + 4 * b:260 + 4 * b], lhsT=ones[:], rhs=st[b][:], start=True, stop=True)
 
         def store(b, h, lo, hi):
             nc.sync.dma_start(out=out[b, 0, h * D:(h + 1) * D, :].rearrange("(p t) k -> p (t k)", p=P, t=4)[:, lo:hi],
@@ -212,10 +204,11 @@ def tile_updateonrightwithselectiveresetonleft_kernel(tc, A1_atop_B1, A2_atop_B2
 
         def correct(b):
             red = smallp.tile([P, 4], F32, name="red")
-            nc.vector.tensor_reduce(out=red[:, 0:2], in_=pst[:, 8 + 4 * b:12 + 4 * b].rearrange("p (a c) -> p a c", a=2),
+            nc.vector.tensor_reduce(out=red[:, 0:2],
+                                    in_=pst[:, 256 + 4 * b:260 + 4 * b].rearrange("p (a c) -> p a c", a=2),
                                     axis=AX.X, op=ALU.add)
             nc.vector.reciprocal(out=red[:, 2:3], in_=red[:, 1:2])
-            nc.vector.scalar_tensor_tensor(out=red[:, 3:4], in0=red[:, 0:1], scalar=kn[:, b:b + 1], in1=red[:, 2:3],
+            nc.vector.scalar_tensor_tensor(out=red[:, 3:4], in0=red[:, 0:1], scalar=sc[b][:, 8:9], in1=red[:, 2:3],
                                            op0=ALU.mult, op1=ALU.mult)
             pieces = 2 if b == B - 1 else 1
             w = 4 * D // pieces
@@ -225,43 +218,55 @@ def tile_updateonrightwithselectiveresetonleft_kernel(tc, A1_atop_B1, A2_atop_B2
                                                op0=ALU.mult, op1=ALU.add)
                 store(b, 0, i * w, (i + 1) * w)
 
+        load(0)
+        load(1)
+        stats_vector(0)
+        stats_tensor(0)
+        stats_chain(0)
         for r in range(B + 1):
             tb = r
             mb = r - 1
+            sb = r + 1
+            if r + 2 < B:
+                load(r + 2)
             if tb < B:
                 alloc_codes(tb)
             for s in range(4):
-                if s == 0 and mb >= 0:
-                    quantise(mb, "g", 0, 1)
-                    quantise(mb, "g", 1, 1)
                 if mb >= 0:
                     mx_tile(mb, 2 * s)
                     mx_tile(mb, 2 * s + 1)
-                    if s == 3:
-                        dot_sum(mb)
                     if s == 2 and mb == B - 1:
                         store(mb, 1, 0, 2 * D)
                 if tb < B:
                     for i in range(3 * s, 3 * s + 3):
                         transpose_bank(tb, i)
-                if mb >= 0 and s == 1:
-                    dot_half(mb, 0)
-                if mb >= 0 and s == 2:
-                    dot_half(mb, 1)
-                if tb < B:
-                    if s == 0:
+                if s == 0:
+                    if 1 <= tb < B:
+                        stats_chain(tb)
+                    if tb < B:
                         quantise(tb, "a", 0, 0)
-                    if s == 1:
+                if s == 1:
+                    if mb >= 0:
+                        dot_half(mb, 0)
+                    if tb < B:
                         quantise(tb, "a", 1, 0)
                         quantise(tb, "g", 0, 0)
-                    if s == 2:
+                    if sb < B:
+                        stats_vector(sb)
+                if s == 2:
+                    if mb >= 0:
+                        dot_half(mb, 1)
+                    if tb < B:
                         quantise(tb, "g", 1, 0)
-                if r == 0 and s == 1:
-                    stat_chain()
-                if mb >= 0 and s == 3:
-                    store(mb, 1, 2 * D if mb == B - 1 else 0, 4 * D)
-                    correct(mb)
-                if tb < B and s == 3:
-                    hits(tb)
-            if r == 0:
-                load_mm(3)
+                        hits(tb)
+                if s == 3:
+                    if mb >= 0:
+                        dot_sum(mb)
+                        store(mb, 1, 2 * D if mb == B - 1 else 0, 4 * D)
+                    if sb < B:
+                        stats_tensor(sb)
+                    if tb < B:
+                        quantise(tb, "g", 0, 1)
+                        quantise(tb, "g", 1, 1)
+                    if mb >= 0:
+                        correct(mb)

@@ -21,6 +21,7 @@ P = 128
 FLOPS = 2 * B * (2 * D) * D * (N * D)
 BYTES = B * (2 * D * D * 2 + N * D * D * 2 + N * 2 * D * D * 2 + 2 * D * D * 4)
 MANUAL = False
+NZ_ON_VECTOR = (2,)
 
 
 def tile_updateonrightwithselectiveresetonleft_kernel(tc, A1_atop_B1, A2_atop_B2, grad_out, out):
@@ -51,6 +52,7 @@ def tile_updateonrightwithselectiveresetonleft_kernel(tc, A1_atop_B1, A2_atop_B2
         junk = const.tile([P, 2 * D], F32, name="junk")
         junkb = const.tile([P, 4 * D], BF16, name="junkb")
         junka = const.tile([P, D], BF16, name="junka")
+        junks = const.tile([P, 4 * D], BF16, name="junks")
         pst = statp.tile([P, D], F32, name="pst")
 
         a1 = {}
@@ -59,6 +61,7 @@ def tile_updateonrightwithselectiveresetonleft_kernel(tc, A1_atop_B1, A2_atop_B2
         a2 = {}
         g = {}
         loc = {}
+        nzp = {}
         tot = {}
         sc = {}
         grp = {}
@@ -67,10 +70,10 @@ def tile_updateonrightwithselectiveresetonleft_kernel(tc, A1_atop_B1, A2_atop_B2
         osb = {}
 
         def load(b):
-            a1[b] = a1p.tile([P, 4 * D], BF16, name="a1")
-            nc.sync.dma_start(out=a1[b][:], in_=A1_atop_B1[b, 0, 0:D, :].rearrange("(p t) j -> p (t j)", p=P, t=4))
             b1[b] = b1p.tile([P, 4 * D], BF16, name="b1")
             nc.sync.dma_start(out=b1[b][:], in_=A1_atop_B1[b, 0, D:2 * D, :].rearrange("(p t) j -> p (t j)", p=P, t=4))
+            a1[b] = a1p.tile([P, 4 * D], BF16, name="a1")
+            nc.sync.dma_start(out=a1[b][:], in_=A1_atop_B1[b, 0, 0:D, :].rearrange("(p t) j -> p (t j)", p=P, t=4))
             for n in range(N):
                 a2[b, n] = a2p.tile([P, 4 * D], BF16, name="a2")
                 nc.sync.dma_start(
@@ -86,13 +89,17 @@ def tile_updateonrightwithselectiveresetonleft_kernel(tc, A1_atop_B1, A2_atop_B2
 
         def stats_vector(b):
             wt[b] = wtp.tile([P, 4 * D], BF16, name="wt")
-            loc[b] = smallp.tile([P, 2], F32, name="loc")
+            loc[b] = smallp.tile([P, 1], F32, name="loc")
+            nzp[b] = smallp.tile([P, 1], F32, name="nzp")
+            if b in NZ_ON_VECTOR:
+                nc.vector.tensor_scalar(out=junkb[:], in0=b1[b][:], scalar1=0.0, scalar2=None, op0=ALU.not_equal,
+                                        op1=ALU.max, accum_out=nzp[b][:])
+            else:
+                nc.scalar.activation(out=junks[:], in_=b1[b][:], func=ACTF.Abs, accum_out=nzp[b][:])
             nc.vector.tensor_scalar(out=wt[b][:].bitcast(I32), in0=a1[b][:].bitcast(I32), scalar1=0x7FFF7FFF,
                                     scalar2=None, op0=ALU.bitwise_and)
             nc.vector.tensor_scalar(out=junkb[:], in0=wt[b][:], scalar1=1.0, scalar2=None, op0=ALU.mult,
                                     op1=ALU.max, accum_out=loc[b][:, 0:1])
-            nc.vector.tensor_scalar(out=junkb[:], in0=b1[b][:], scalar1=0.0, scalar2=None, op0=ALU.not_equal,
-                                    op1=ALU.max, accum_out=loc[b][:, 1:2])
 
         def stats_tensor(b):
             ptot = accp.tile([P, D], F32, name="acc")
@@ -100,8 +107,8 @@ def tile_updateonrightwithselectiveresetonleft_kernel(tc, A1_atop_B1, A2_atop_B2
                 nc.tensor.matmul(out=ptot[:], lhsT=onesb[:], rhs=wt[b][:, t * D:(t + 1) * D], start=(t == 0), stop=(t == 3))
             tot[b] = smallp.tile([P, 1], F32, name="tot")
             nc.scalar.activation(out=junka[:], in_=ptot[:], func=ACTF.Copy, accum_out=tot[b][:])
-            for i in range(2):
-                nc.tensor.matmul(out=pst[:, i * P:(i + 1) * P], lhsT=loc[b][:, i:i + 1].to_broadcast([P, P]),
+            for i, v in enumerate((loc[b], nzp[b])):
+                nc.tensor.matmul(out=pst[:, i * P:(i + 1) * P], lhsT=v[:].to_broadcast([P, P]),
                                  rhs=ident[:], start=True, stop=True)
 
         def stats_chain(b):

@@ -20,8 +20,6 @@ D = 512
 P = 128
 FLOPS = 2 * B * (2 * D) * D * (N * D)
 BYTES = B * (2 * D * D * 2 + N * D * D * 2 + N * 2 * D * D * 2 + 2 * D * D * 4)
-MANUAL = False
-NZ_ON_VECTOR = (2,)
 
 
 def tile_updateonrightwithselectiveresetonleft_kernel(tc, A1_atop_B1, A2_atop_B2, grad_out, out):
@@ -30,104 +28,57 @@ def tile_updateonrightwithselectiveresetonleft_kernel(tc, A1_atop_B1, A2_atop_B2
         const = ctx.enter_context(tc.tile_pool(name="const", bufs=1))
         a1p = ctx.enter_context(tc.tile_pool(name="a1p", bufs=4))
         b1p = ctx.enter_context(tc.tile_pool(name="b1p", bufs=3))
-        wtp = ctx.enter_context(tc.tile_pool(name="wtp", bufs=3))
         a2p = ctx.enter_context(tc.tile_pool(name="a2p", bufs=6))
-        gp = ctx.enter_context(tc.tile_pool(name="gp", bufs=6))
-        grpp = ctx.enter_context(tc.tile_pool(name="grpp", bufs=4))
+        gp = ctx.enter_context(tc.tile_pool(name="gp", bufs=12))
+        wtp = ctx.enter_context(tc.tile_pool(name="wtp", bufs=3))
+        hitp = ctx.enter_context(tc.tile_pool(name="hitp", bufs=2))
+        grpp = ctx.enter_context(tc.tile_pool(name="grpp", bufs=6))
         codep = ctx.enter_context(tc.tile_pool(name="codep", bufs=2))
-        op = ctx.enter_context(tc.tile_pool(name="op", bufs=4))
+        op = ctx.enter_context(tc.tile_pool(name="op", bufs=5))
         smallp = ctx.enter_context(tc.tile_pool(name="smallp", bufs=3))
         xtp = ctx.enter_context(tc.psum_pool(name="xtp", bufs=3))
-        accp = ctx.enter_context(tc.psum_pool(name="accp", bufs=4))
+        accp = ctx.enter_context(tc.psum_pool(name="accp", bufs=3))
         statp = ctx.enter_context(tc.psum_pool(name="statp", bufs=1))
-        if MANUAL:
-            ctx.enter_context(tc.manual_schedule())
+        ctx.enter_context(tc.manual_schedule())
 
         ident = const.tile([P, P], F32, name="ident")
         make_identity(nc, ident[:])
         ones = const.tile([P, P], F32, name="ones")
         nc.vector.memset(ones[:], 1.0)
-        onesb = const.tile([P, P], BF16, name="onesb")
+        onesb = const.tile([P, 2], BF16, name="onesb")
         nc.vector.memset(onesb[:], 1.0)
         junk = const.tile([P, 2 * D], F32, name="junk")
-        junkb = const.tile([P, 4 * D], BF16, name="junkb")
-        junka = const.tile([P, D], BF16, name="junka")
-        junks = const.tile([P, 4 * D], BF16, name="junks")
         pst = statp.tile([P, D], F32, name="pst")
+        cst = statp.tile([P, D], F32, name="cst")
 
-        a1 = {}
-        b1 = {}
-        wt = {}
-        a2 = {}
-        g = {}
-        loc = {}
-        nzp = {}
-        tot = {}
-        sc = {}
-        grp = {}
-        codes = {}
-        st = {}
-        osb = {}
+        a1, b1, a2, g = {}, {}, {}, {}
+        wt, hit, sc, dots, part, total = {}, {}, {}, {}, {}, {}
+        grp, codes, osb = {}, {}, {}
 
-        def load(b):
-            b1[b] = b1p.tile([P, 4 * D], BF16, name="b1")
-            nc.sync.dma_start(out=b1[b][:], in_=A1_atop_B1[b, 0, D:2 * D, :].rearrange("(p t) j -> p (t j)", p=P, t=4))
+        def load_a1(b):
             a1[b] = a1p.tile([P, 4 * D], BF16, name="a1")
             nc.sync.dma_start(out=a1[b][:], in_=A1_atop_B1[b, 0, 0:D, :].rearrange("(p t) j -> p (t j)", p=P, t=4))
-            for n in range(N):
-                a2[b, n] = a2p.tile([P, 4 * D], BF16, name="a2")
-                nc.sync.dma_start(
-                    out=a2[b, n][:].rearrange("p (h c) -> p h c", h=2),
-                    in_=A2_atop_B2[b, n, 0:D, :].rearrange("(h p t) j -> p h (t j)", h=2, p=P, t=2),
-                )
-            for n in range(N):
-                g[b, n] = gp.tile([P, 8 * D], BF16, name="g")
-                nc.sync.dma_start(
-                    out=g[b, n][:].rearrange("p (h c) -> p h c", h=2),
-                    in_=grad_out[b, n].rearrange("(h p t) j -> p h (t j)", h=2, p=P, t=4),
-                )
 
-        def stats_vector(b):
-            wt[b] = wtp.tile([P, 4 * D], BF16, name="wt")
-            loc[b] = smallp.tile([P, 1], F32, name="loc")
-            nzp[b] = smallp.tile([P, 1], F32, name="nzp")
-            if b in NZ_ON_VECTOR:
-                nc.vector.tensor_scalar(out=junkb[:], in0=b1[b][:], scalar1=0.0, scalar2=None, op0=ALU.not_equal,
-                                        op1=ALU.max, accum_out=nzp[b][:])
-            else:
-                nc.scalar.activation(out=junks[:], in_=b1[b][:], func=ACTF.Abs, accum_out=nzp[b][:])
-            nc.vector.tensor_scalar(out=wt[b][:].bitcast(I32), in0=a1[b][:].bitcast(I32), scalar1=0x7FFF7FFF,
-                                    scalar2=None, op0=ALU.bitwise_and)
-            nc.vector.tensor_scalar(out=junkb[:], in0=wt[b][:], scalar1=1.0, scalar2=None, op0=ALU.mult,
-                                    op1=ALU.max, accum_out=loc[b][:, 0:1])
+        def load_b1(b):
+            b1[b] = b1p.tile([P, 4 * D], BF16, name="b1")
+            nc.sync.dma_start(out=b1[b][:], in_=A1_atop_B1[b, 0, D:2 * D, :].rearrange("(p t) j -> p (t j)", p=P, t=4))
 
-        def stats_tensor(b):
-            ptot = accp.tile([P, D], F32, name="acc")
-            for t in range(4):
-                nc.tensor.matmul(out=ptot[:], lhsT=onesb[:], rhs=wt[b][:, t * D:(t + 1) * D], start=(t == 0), stop=(t == 3))
-            tot[b] = smallp.tile([P, 1], F32, name="tot")
-            nc.scalar.activation(out=junka[:], in_=ptot[:], func=ACTF.Copy, accum_out=tot[b][:])
-            for i, v in enumerate((loc[b], nzp[b])):
-                nc.tensor.matmul(out=pst[:, i * P:(i + 1) * P], lhsT=v[:].to_broadcast([P, P]),
-                                 rhs=ident[:], start=True, stop=True)
+        def load_a2(b, n, halves=1):
+            a2[b, n] = a2p.tile([P, 4 * D], BF16, name="a2")
+            dst = a2[b, n][:].rearrange("p (h c) -> p h c", h=2)
+            src = A2_atop_B2[b, n, 0:D, :].rearrange("(h p t) j -> p h (t j)", h=2, p=P, t=2)
+            for i in range(halves):
+                hs = slice(i * 2 // halves, (i + 1) * 2 // halves)
+                nc.sync.dma_start(out=dst[:, hs, :], in_=src[:, hs, :])
 
-        def stats_chain(b):
-            s = smallp.tile([P, 10], F32, name="sc")
-            sc[b] = s
-            nc.vector.tensor_reduce(out=s[:, 0:2], in_=pst[:, 0:2 * P].rearrange("p (a c) -> p a c", a=2), axis=AX.X,
-                                    op=ALU.max)
-            nc.vector.tensor_scalar(out=s[:, 2:3], in0=s[:, 1:2], scalar1=0.0, scalar2=tot[b][:], op0=ALU.is_equal,
-                                    op1=ALU.mult)
-            nc.vector.tensor_scalar(out=s[:, 3:4], in0=s[:, 2:3], scalar1=float(D * D), scalar2=None, op0=ALU.is_le)
-            nc.vector.tensor_scalar(out=s[:, 4:5], in0=s[:, 0:1], scalar1=1.0, scalar2=None, op0=ALU.max)
-            nc.vector.reciprocal(out=s[:, 5:6], in_=s[:, 4:5])
-            nc.vector.tensor_scalar(out=s[:, 6:7], in0=s[:, 3:4], scalar1=0.0, scalar2=s[:, 5:6], op0=ALU.is_equal,
-                                    op1=ALU.mult)
-            nc.vector.tensor_tensor(out=s[:, 7:8], in0=s[:, 6:7], in1=s[:, 3:4], op=ALU.add)
-            nc.vector.scalar_tensor_tensor(out=s[:, 8:9], in0=s[:, 6:7], scalar=-1.0, in1=s[:, 5:6], op0=ALU.mult,
-                                           op1=ALU.mult)
+        def load_g(b, n, h):
+            g[b, n, h] = gp.tile([P, 4 * D], BF16, name="g")
+            nc.sync.dma_start(out=g[b, n, h][:],
+                              in_=grad_out[b, n, h * D:(h + 1) * D, :].rearrange("(p t) j -> p (t j)", p=P, t=4))
 
         def alloc_codes(b):
+            if b >= B:
+                return
             codes[b] = (
                 codep.tile([P, N * 2 * D], U32, name="gc", align_bytes=64),
                 codep.tile([P, N * 2 * D], U8, name="gs", align_bytes=64),
@@ -135,145 +86,293 @@ def tile_updateonrightwithselectiveresetonleft_kernel(tc, A1_atop_B1, A2_atop_B2
                 codep.tile([P, N * D], U8, name="as_", align_bytes=64),
             )
 
-        BANKS = [("a", 0, 0, 0), ("a", 0, 1, 0), ("a", 1, 0, 0), ("a", 1, 1, 0),
-                 ("g", 0, 0, 0), ("g", 0, 0, 1), ("g", 1, 0, 0), ("g", 1, 0, 1),
-                 ("g", 0, 1, 0), ("g", 0, 1, 1), ("g", 1, 1, 0), ("g", 1, 1, 1)]
-
-        def transpose_bank(b, i):
-            kind, n, h, pr = BANKS[i]
+        def turn(kind, b, n, h, i):
+            if b >= B:
+                return
+            src = (a2[b, n] if kind == "a" else g[b, n, h])[:].bitcast(F32)
+            if i == 0:
+                grp[kind, b, n, h] = grpp.tile([P, 4 * D], BF16, name="grp", align_bytes=64)
             xt = xtp.tile([P, 4, P], F32, name="xt")
-            if kind == "a":
-                src = a2[b, n][:].bitcast(F32)
-                base = h * 512
-                key = (b, "a", n)
-                first = h == 0
-            else:
-                src = g[b, n][:].bitcast(F32)
-                base = h * 1024 + pr * 512
-                key = (b, "g", n, h)
-                first = pr == 0
             for s in range(4):
-                nc.tensor.transpose(xt[:, s, :], src[:, base + s * P:base + (s + 1) * P], ident[:])
-            if first:
-                grp[key] = grpp.tile([P, 4 * D], BF16, name="grp", align_bytes=64)
-            words = grp[key][:].bitcast(F32)
+                lo = i * 512 + s * P
+                nc.tensor.transpose(xt[:, s, :], src[:, lo:lo + P], ident[:])
+            half = grp[kind, b, n, h][:].bitcast(F32)[:, i * 512:(i + 1) * 512]
             if kind == "a":
-                nc.scalar.copy(out=words[:, h * 512:(h + 1) * 512].rearrange("q (r s) -> q r s", s=4),
-                               in_=xt[:].rearrange("q s r -> q r s"))
+                nc.scalar.copy(out=half.rearrange("q (r s) -> q r s", s=4), in_=xt[:].rearrange("q s r -> q r s"))
             else:
-                nc.scalar.copy(out=words[:, pr * 512:(pr + 1) * 512].rearrange("q (t r u) -> q t r u", t=2, u=2),
+                nc.scalar.copy(out=half.rearrange("q (t r u) -> q t r u", t=2, u=2),
                                in_=xt[:].rearrange("q (t u) r -> q t r u", t=2, u=2))
 
-        def quantise(b, kind, n, h):
+        def quantise(kind, b, n, h=0):
+            if b >= B:
+                return
             gc, gs, ac, as_ = codes[b]
             if kind == "a":
                 cols = slice(n * D, (n + 1) * D)
-                nc.vector.quantize_mx(out=ac[:, cols].bitcast(E4), scales=as_[:, cols], in_=grp[b, "a", n][:])
+                nc.vector.quantize_mx(out=ac[:, cols].bitcast(E4), scales=as_[:, cols], in_=grp[kind, b, n, h][:])
             else:
                 lo = n * 2 * D + h * D
                 cols = slice(lo, lo + D)
-                nc.vector.quantize_mx(out=gc[:, cols].bitcast(E5), scales=gs[:, cols], in_=grp[b, "g", n, h][:])
+                nc.vector.quantize_mx(out=gc[:, cols].bitcast(E5), scales=gs[:, cols], in_=grp[kind, b, n, h][:])
 
-        def mx_tile(b, ti):
+        def multiply(b, h, t):
+            if b < 0:
+                return
             gc, gs, ac, as_ = codes[b]
-            h = ti // 4
-            t = ti % 4
             if t == 0:
                 osb[b, h] = op.tile([P, 4 * D], F32, name="osb")
+            scale = sc[b][:, 8:9] if h == 0 else sc[b][:, 1:2]
             acc = accp.tile([P, D], F32, name="acc")
             for n in range(N):
-                lo = n * 2 * D + ti * P
+                lo = n * 2 * D + h * D + t * P
                 nc.tensor.matmul_mx(out=acc[:], lhsT=gc[:, lo:lo + P].bitcast(E5), lhsT_scale=gs[:, lo:lo + P],
                                     rhs=ac[:, n * D:(n + 1) * D].bitcast(E4), rhs_scale=as_[:, n * D:(n + 1) * D],
                                     start=(n == 0), stop=(n == N - 1))
-            scale = sc[b][:, 7:8] if h == 0 else sc[b][:, 3:4]
             nc.scalar.activation(out=osb[b, h][:, t * D:(t + 1) * D], in_=acc[:], func=ACTF.Copy, scale=scale)
 
+        def abs_a1(b):
+            if b >= B:
+                return
+            wt[b] = wtp.tile([P, 4 * D], BF16, name="wt")
+            hit[b] = hitp.tile([P, 4 * D], BF16, name="hit")
+            nc.vector.tensor_scalar(out=wt[b][:].bitcast(I32), in0=a1[b][:].bitcast(I32), scalar1=0x7FFF7FFF,
+                                    scalar2=None, op0=ALU.bitwise_and)
+
+        def nonzero_b1(b):
+            if b >= B:
+                return
+            nc.vector.tensor_scalar(out=b1[b][:], in0=b1[b][:], scalar1=0.0, scalar2=None, op0=ALU.not_equal)
+
+        def row_max(b):
+            if b >= B:
+                return
+            sc[b] = smallp.tile([P, 12], F32, name="sc")
+            nc.vector.tensor_scalar(out=hit[b][:], in0=wt[b][:], scalar1=1.0, scalar2=None, op0=ALU.mult,
+                                    op1=ALU.max, accum_out=sc[b][:, 11:12])
+
+        def column_sums(b, x, i):
+            if b >= B:
+                return
+            lo = 32 * b + 2 * i
+            for c in range(16):
+                nc.tensor.matmul(out=pst[:, lo:lo + 2], lhsT=x[b][:, c * P:(c + 1) * P], rhs=onesb[:], start=(c == 0),
+                                 stop=(c == 15))
+
+        def spread_max(b):
+            if b >= B:
+                return
+            nc.tensor.matmul(out=pst[:, P:2 * P], lhsT=sc[b][:, 11:12].to_broadcast([P, P]), rhs=ident[:], start=True,
+                             stop=True)
+
+        def whole_max(b):
+            if b >= B:
+                return
+            nc.vector.tensor_reduce(out=sc[b][:, 0:1], in_=pst[:, P:2 * P], axis=AX.X, op=ALU.max)
+
         def hits(b):
-            st[b] = smallp.tile([P, 4], F32, name="st")
-            for hf in range(2):
-                cols = slice(hf * 2 * D, (hf + 1) * 2 * D)
-                nc.vector.tensor_scalar(out=wt[b][:, cols], in0=wt[b][:, cols], scalar1=sc[b][:, 0:1], scalar2=None,
-                                        op0=ALU.is_equal, op1=ALU.add, accum_out=st[b][:, 2 + hf:3 + hf])
-            nc.vector.tensor_tensor(out=wt[b][:], in0=wt[b][:], in1=a1[b][:], op=ALU.mult)
+            if b >= B:
+                return
+            nc.vector.tensor_scalar(out=hit[b][:], in0=wt[b][:], scalar1=sc[b][:, 0:1], scalar2=None, op0=ALU.is_equal)
 
-        def dot_half(b, hf):
-            cols = slice(hf * 2 * D, (hf + 1) * 2 * D)
+        def signed_hits(b):
+            if b >= B:
+                return
+            nc.vector.tensor_tensor(out=wt[b][:], in0=hit[b][:], in1=a1[b][:], op=ALU.mult)
+
+        def partials(b):
+            if b >= B:
+                return
+            part[b] = smallp.tile([P, 6], F32, name="part")
+            nc.scalar.copy(out=part[b][:], in_=pst[:, 32 * b:32 * b + 6])
+
+        def sum_partials(b):
+            if b >= B:
+                return
+            nc.tensor.matmul(out=pst[:, 32 * b + 8:32 * b + 14], lhsT=ones[:], rhs=part[b][:], start=True, stop=True)
+
+        def totals(b):
+            if b >= B:
+                return
+            total[b] = smallp.tile([P, 6], F32, name="total")
+            nc.scalar.copy(out=total[b][:], in_=pst[:, 32 * b + 8:32 * b + 14])
+
+        def decide(b):
+            if b >= B:
+                return
+            s, t_ = sc[b], total[b]
+            nc.gpsimd.tensor_scalar(out=s[:, 2:3], in0=t_[:, 2:3], scalar1=0.0, scalar2=t_[:, 0:1], op0=ALU.is_equal,
+                                    op1=ALU.mult)
+            nc.gpsimd.tensor_scalar(out=s[:, 1:2], in0=s[:, 2:3], scalar1=float(D * D), scalar2=None, op0=ALU.is_le)
+            nc.gpsimd.tensor_scalar(out=s[:, 3:4], in0=s[:, 2:3], scalar1=float(D * D), scalar2=None, op0=ALU.is_gt)
+            nc.gpsimd.tensor_scalar(out=s[:, 4:5], in0=s[:, 3:4], scalar1=s[:, 0:1], scalar2=s[:, 1:2], op0=ALU.mult,
+                                    op1=ALU.add)
+            nc.gpsimd.tensor_scalar(out=s[:, 5:6], in0=s[:, 4:5], scalar1=s[:, 4:5], scalar2=t_[:, 4:5], op0=ALU.mult,
+                                    op1=ALU.mult)
+
+        def scales(b):
+            if b >= B:
+                return
+            nc.vector.reciprocal(out=sc[b][:, 8:10], in_=sc[b][:, 4:6])
+
+        def factor(b):
+            if b >= B:
+                return
+            s = sc[b]
+            nc.gpsimd.tensor_scalar(out=s[:, 10:11], in0=s[:, 9:10], scalar1=s[:, 3:4], scalar2=-1.0, op0=ALU.mult,
+                                    op1=ALU.mult)
+
+        def dot(b, i):
+            if i == 0:
+                dots[b] = smallp.tile([P, 2], F32, name="dots")
+            cols = slice(i * 2 * D, (i + 1) * 2 * D)
             nc.vector.scalar_tensor_tensor(out=junk[:], in0=osb[b, 0][:, cols], scalar=1.0, in1=a1[b][:, cols],
-                                           op0=ALU.mult, op1=ALU.mult, accum_out=st[b][:, hf:hf + 1])
+                                           op0=ALU.mult, op1=ALU.mult, accum_out=dots[b][:, i:i + 1])
 
-        def dot_sum(b):
-            nc.tensor.matmul(out=pst[:, 256 + 4 * b:260 + 4 * b], lhsT=ones[:], rhs=st[b][:], start=True, stop=True)
+        def coefficient(b):
+            for i in range(2):
+                nc.tensor.matmul(out=cst[:, b:b + 1], lhsT=sc[b][:, 10:11].to_broadcast([P, P]),
+                                 rhs=dots[b][:, i:i + 1], start=(i == 0), stop=(i == 1))
+
+        def correct(b, lo, hi):
+            cols = slice(lo, hi)
+            nc.vector.scalar_tensor_tensor(out=osb[b, 0][:, cols], in0=wt[b][:, cols],
+                                           scalar=cst[:, b:b + 1], in1=osb[b, 0][:, cols],
+                                           op0=ALU.mult, op1=ALU.add)
 
         def store(b, h, lo, hi):
             nc.sync.dma_start(out=out[b, 0, h * D:(h + 1) * D, :].rearrange("(p t) k -> p (t k)", p=P, t=4)[:, lo:hi],
                               in_=osb[b, h][:, lo:hi])
 
-        def correct(b):
-            red = smallp.tile([P, 4], F32, name="red")
-            nc.vector.tensor_reduce(out=red[:, 0:2],
-                                    in_=pst[:, 256 + 4 * b:260 + 4 * b].rearrange("p (a c) -> p a c", a=2),
-                                    axis=AX.X, op=ALU.add)
-            nc.vector.reciprocal(out=red[:, 2:3], in_=red[:, 1:2])
-            nc.vector.scalar_tensor_tensor(out=red[:, 3:4], in0=red[:, 0:1], scalar=sc[b][:, 8:9], in1=red[:, 2:3],
-                                           op0=ALU.mult, op1=ALU.mult)
-            pieces = 2 if b == B - 1 else 1
-            w = 4 * D // pieces
-            for i in range(pieces):
-                nc.vector.scalar_tensor_tensor(out=osb[b, 0][:, i * w:(i + 1) * w], in0=wt[b][:, i * w:(i + 1) * w],
-                                               scalar=red[:, 3:4], in1=osb[b, 0][:, i * w:(i + 1) * w],
-                                               op0=ALU.mult, op1=ALU.add)
-                store(b, 0, i * w, (i + 1) * w)
+        def load_entry(b):
+            if b >= B:
+                return
+            load_a2(b, 0)
+            load_a2(b, 1)
+            load_a1(b)
+            load_b1(b)
+            for h in range(2):
+                for n in range(N):
+                    load_g(b, n, h)
 
-        load(0)
-        load(1)
-        stats_vector(0)
-        stats_tensor(0)
-        stats_chain(0)
-        for r in range(B + 1):
-            tb = r
-            mb = r - 1
-            sb = r + 1
-            if r + 2 < B:
-                load(r + 2)
-            if tb < B:
-                alloc_codes(tb)
-            for s in range(4):
-                if mb >= 0:
-                    mx_tile(mb, 2 * s)
-                    mx_tile(mb, 2 * s + 1)
-                    if s == 2 and mb == B - 1:
-                        store(mb, 1, 0, 2 * D)
-                if tb < B:
-                    for i in range(3 * s, 3 * s + 3):
-                        transpose_bank(tb, i)
-                if s == 0:
-                    if 1 <= tb < B:
-                        stats_chain(tb)
-                    if tb < B:
-                        quantise(tb, "a", 0, 0)
-                if s == 1:
-                    if mb >= 0:
-                        dot_half(mb, 0)
-                    if tb < B:
-                        quantise(tb, "a", 1, 0)
-                        quantise(tb, "g", 0, 0)
-                    if sb < B:
-                        stats_vector(sb)
-                if s == 2:
-                    if mb >= 0:
-                        dot_half(mb, 1)
-                    if tb < B:
-                        quantise(tb, "g", 1, 0)
-                        hits(tb)
-                if s == 3:
-                    if mb >= 0:
-                        dot_sum(mb)
-                        store(mb, 1, 2 * D if mb == B - 1 else 0, 4 * D)
-                    if sb < B:
-                        stats_tensor(sb)
-                    if tb < B:
-                        quantise(tb, "g", 0, 1)
-                        quantise(tb, "g", 1, 1)
-                    if mb >= 0:
-                        correct(mb)
+        load_a2(0, 0, halves=2)
+        load_a1(0)
+        load_a2(0, 1)
+        load_g(0, 0, 0)
+        load_g(0, 1, 0)
+        load_b1(0)
+        load_g(0, 0, 1)
+        load_g(0, 1, 1)
+        load_a1(1)
+        load_b1(1)
+        load_a2(1, 0)
+        load_a2(1, 1)
+        load_g(1, 0, 0)
+        load_g(1, 1, 0)
+        load_a1(2)
+        load_b1(2)
+        load_g(1, 0, 1)
+        load_g(1, 1, 1)
+        load_a2(2, 0)
+        load_a2(2, 1)
+        for h in range(2):
+            for n in range(N):
+                load_g(2, n, h)
+        alloc_codes(0)
+        turn("a", 0, 0, 0, 0)
+        turn("a", 0, 0, 0, 1)
+        abs_a1(0)
+        row_max(0)
+        quantise("a", 0, 0)
+        turn("a", 0, 1, 0, 0)
+        turn("a", 0, 1, 0, 1)
+        column_sums(0, wt, 0)
+        spread_max(0)
+        turn("g", 0, 0, 0, 0)
+        whole_max(0)
+        turn("g", 0, 0, 0, 1)
+        quantise("a", 0, 1)
+        hits(0)
+        turn("g", 0, 1, 0, 0)
+        turn("g", 0, 1, 0, 1)
+        column_sums(0, hit, 2)
+        quantise("g", 0, 0, 0)
+        nonzero_b1(0)
+        quantise("g", 0, 1, 0)
+        turn("g", 0, 0, 1, 0)
+        column_sums(0, b1, 1)
+        partials(0)
+        turn("g", 0, 0, 1, 1)
+        sum_partials(0)
+        totals(0)
+        decide(0)
+        signed_hits(0)
+        turn("g", 0, 1, 1, 0)
+        scales(0)
+        factor(0)
+        quantise("g", 0, 0, 1)
+        turn("g", 0, 1, 1, 1)
+        abs_a1(1)
+        row_max(1)
+        nonzero_b1(1)
+
+        for b in range(B):
+            last = b == B - 1
+            multiply(b, 0, 0)
+            quantise("g", b, 1, 1)
+            multiply(b, 0, 1)
+            if b == 0:
+                load_a1(3)
+                load_b1(3)
+                load_a2(3, 0)
+                load_a2(3, 1)
+                for h in range(2):
+                    for n in range(N):
+                        load_g(3, n, h)
+            column_sums(b + 1, wt, 0)
+            spread_max(b + 1)
+            multiply(b, 0, 2)
+            dot(b, 0)
+            multiply(b, 0, 3)
+            column_sums(b + 1, b1, 1)
+            whole_max(b + 1)
+            alloc_codes(b + 1)
+            turn("a", b + 1, 0, 0, 0)
+            dot(b, 1)
+            turn("a", b + 1, 0, 0, 1)
+            hits(b + 1)
+            turn("a", b + 1, 1, 0, 0)
+            quantise("a", b + 1, 0)
+            turn("a", b + 1, 1, 0, 1)
+            multiply(b, 1, 0)
+            quantise("a", b + 1, 1)
+            multiply(b, 1, 1)
+            coefficient(b)
+            abs_a1(b + 2)
+            multiply(b, 1, 2)
+            column_sums(b + 1, hit, 2)
+            partials(b + 1)
+            correct(b, 0, 2 * D)
+            store(b, 0, 0, 2 * D)
+            multiply(b, 1, 3)
+            store(b, 1, 0, 4 * D)
+            turn("g", b + 1, 0, 0, 0)
+            sum_partials(b + 1)
+            totals(b + 1)
+            decide(b + 1)
+            correct(b, 2 * D, 4 * D)
+            store(b, 0, 2 * D, 4 * D)
+            turn("g", b + 1, 0, 0, 1)
+            turn("g", b + 1, 1, 0, 0)
+            quantise("g", b + 1, 0, 0)
+            turn("g", b + 1, 1, 0, 1)
+            scales(b + 1)
+            factor(b + 1)
+            nonzero_b1(b + 2)
+            quantise("g", b + 1, 1, 0)
+            turn("g", b + 1, 0, 1, 0)
+            row_max(b + 2)
+            turn("g", b + 1, 0, 1, 1)
+            turn("g", b + 1, 1, 1, 0)
+            quantise("g", b + 1, 0, 1)
+            turn("g", b + 1, 1, 1, 1)
+            signed_hits(b + 1)

@@ -196,30 +196,27 @@ def tile_updateonrightwithselectiveresetonleft_kernel(tc, A1_atop_B1, A2_atop_B2
             total[b] = smallp.tile([P, 6], F32, name="total")
             nc.scalar.copy(out=total[b][:], in_=pst[:, 32 * b + 8:32 * b + 14])
 
-        def decide(b):
+        def decide(b, step):
             if b >= B:
                 return
             s, t_ = sc[b], total[b]
-            nc.gpsimd.tensor_scalar(out=s[:, 2:3], in0=t_[:, 2:3], scalar1=0.0, scalar2=t_[:, 0:1], op0=ALU.is_equal,
-                                    op1=ALU.mult)
-            nc.gpsimd.tensor_scalar(out=s[:, 1:2], in0=s[:, 2:3], scalar1=float(D * D), scalar2=None, op0=ALU.is_le)
-            nc.gpsimd.tensor_scalar(out=s[:, 3:4], in0=s[:, 2:3], scalar1=float(D * D), scalar2=None, op0=ALU.is_gt)
-            nc.gpsimd.tensor_scalar(out=s[:, 4:5], in0=s[:, 3:4], scalar1=s[:, 0:1], scalar2=s[:, 1:2], op0=ALU.mult,
-                                    op1=ALU.add)
-            nc.gpsimd.tensor_scalar(out=s[:, 5:6], in0=s[:, 4:5], scalar1=s[:, 4:5], scalar2=t_[:, 4:5], op0=ALU.mult,
-                                    op1=ALU.mult)
-
-        def scales(b):
-            if b >= B:
-                return
-            nc.vector.reciprocal(out=sc[b][:, 8:10], in_=sc[b][:, 4:6])
-
-        def factor(b):
-            if b >= B:
-                return
-            s = sc[b]
-            nc.gpsimd.tensor_scalar(out=s[:, 10:11], in0=s[:, 9:10], scalar1=s[:, 3:4], scalar2=-1.0, op0=ALU.mult,
-                                    op1=ALU.mult)
+            if step == 0:
+                nc.vector.tensor_scalar(out=s[:, 2:3], in0=t_[:, 2:3], scalar1=0.0, scalar2=t_[:, 0:1],
+                                        op0=ALU.is_equal, op1=ALU.mult)
+            if step == 1:
+                nc.vector.tensor_scalar(out=s[:, 3:4], in0=s[:, 2:3], scalar1=float(D * D), scalar2=None, op0=ALU.is_gt)
+                nc.vector.tensor_scalar(out=s[:, 1:2], in0=s[:, 2:3], scalar1=float(D * D), scalar2=None, op0=ALU.is_le)
+            if step == 2:
+                nc.vector.tensor_scalar(out=s[:, 4:5], in0=s[:, 3:4], scalar1=s[:, 0:1], scalar2=1.0, op0=ALU.mult,
+                                        op1=ALU.max)
+            if step == 3:
+                nc.vector.tensor_scalar(out=s[:, 5:6], in0=s[:, 4:5], scalar1=s[:, 4:5], scalar2=t_[:, 4:5],
+                                        op0=ALU.mult, op1=ALU.mult)
+            if step == 4:
+                nc.vector.reciprocal(out=s[:, 8:10], in_=s[:, 4:6])
+            if step == 5:
+                nc.vector.tensor_scalar(out=s[:, 10:11], in0=s[:, 9:10], scalar1=s[:, 3:4], scalar2=-1.0, op0=ALU.mult,
+                                        op1=ALU.mult)
 
         def dot(b, i):
             if i == 0:
@@ -260,9 +257,9 @@ def tile_updateonrightwithselectiveresetonleft_kernel(tc, A1_atop_B1, A2_atop_B2
         load_g(0, 0, 0)
         load_g(0, 1, 0)
         load_b1(0)
+        load_a1(1)
         load_g(0, 0, 1)
         load_g(0, 1, 1)
-        load_a1(1)
         load_b1(1)
         load_a2(1, 0)
         load_a2(1, 1)
@@ -295,8 +292,8 @@ def tile_updateonrightwithselectiveresetonleft_kernel(tc, A1_atop_B1, A2_atop_B2
         turn("g", 0, 1, 0, 0)
         turn("g", 0, 1, 0, 1)
         column_sums(0, hit, 2)
-        quantise("g", 0, 0, 0)
         nonzero_b1(0)
+        quantise("g", 0, 0, 0)
         quantise("g", 0, 1, 0)
         turn("g", 0, 0, 1, 0)
         column_sums(0, b1, 1)
@@ -304,22 +301,28 @@ def tile_updateonrightwithselectiveresetonleft_kernel(tc, A1_atop_B1, A2_atop_B2
         turn("g", 0, 0, 1, 1)
         sum_partials(0)
         totals(0)
-        decide(0)
-        signed_hits(0)
         turn("g", 0, 1, 1, 0)
-        scales(0)
-        factor(0)
-        quantise("g", 0, 0, 1)
-        turn("g", 0, 1, 1, 1)
         abs_a1(1)
+        decide(0, 0)
+        quantise("g", 0, 0, 1)
+        decide(0, 1)
+        decide(0, 2)
         row_max(1)
+        decide(0, 3)
+        turn("g", 0, 1, 1, 1)
         nonzero_b1(1)
+        decide(0, 4)
+        signed_hits(0)
+        decide(0, 5)
 
         for b in range(B):
             last = b == B - 1
             multiply(b, 0, 0)
             quantise("g", b, 1, 1)
             multiply(b, 0, 1)
+            column_sums(b + 1, wt, 0)
+            spread_max(b + 1)
+            whole_max(b + 1)
             if b == 0:
                 load_a1(3)
                 load_b1(3)
@@ -328,51 +331,51 @@ def tile_updateonrightwithselectiveresetonleft_kernel(tc, A1_atop_B1, A2_atop_B2
                 for h in range(2):
                     for n in range(N):
                         load_g(3, n, h)
-            column_sums(b + 1, wt, 0)
-            spread_max(b + 1)
-            multiply(b, 0, 2)
-            dot(b, 0)
-            multiply(b, 0, 3)
-            column_sums(b + 1, b1, 1)
-            whole_max(b + 1)
             alloc_codes(b + 1)
             turn("a", b + 1, 0, 0, 0)
-            dot(b, 1)
+            dot(b, 0)
             turn("a", b + 1, 0, 0, 1)
             hits(b + 1)
             turn("a", b + 1, 1, 0, 0)
+            multiply(b, 0, 2)
             quantise("a", b + 1, 0)
+            multiply(b, 0, 3)
+            column_sums(b + 1, b1, 1)
             turn("a", b + 1, 1, 0, 1)
-            multiply(b, 1, 0)
-            quantise("a", b + 1, 1)
-            multiply(b, 1, 1)
-            coefficient(b)
-            abs_a1(b + 2)
-            multiply(b, 1, 2)
+            dot(b, 1)
+            turn("g", b + 1, 0, 0, 0)
             column_sums(b + 1, hit, 2)
             partials(b + 1)
-            correct(b, 0, 2 * D)
-            store(b, 0, 0, 2 * D)
-            multiply(b, 1, 3)
-            store(b, 1, 0, 4 * D)
-            turn("g", b + 1, 0, 0, 0)
+            abs_a1(b + 2)
+            turn("g", b + 1, 0, 0, 1)
+            quantise("a", b + 1, 1)
+            multiply(b, 1, 0)
+            multiply(b, 1, 1)
             sum_partials(b + 1)
             totals(b + 1)
-            decide(b + 1)
+            quantise("g", b + 1, 0, 0)
+            nonzero_b1(b + 2)
+            decide(b + 1, 0)
+            turn("g", b + 1, 1, 0, 0)
+            row_max(b + 2)
+            decide(b + 1, 1)
+            turn("g", b + 1, 1, 0, 1)
+            coefficient(b)
+            turn("g", b + 1, 0, 1, 0)
+            quantise("g", b + 1, 1, 0)
+            decide(b + 1, 2)
+            multiply(b, 1, 2)
+            correct(b, 0, 2 * D)
+            store(b, 0, 0, 2 * D)
+            decide(b + 1, 3)
+            multiply(b, 1, 3)
+            store(b, 1, 0, 4 * D)
+            turn("g", b + 1, 0, 1, 1)
             correct(b, 2 * D, 4 * D)
             store(b, 0, 2 * D, 4 * D)
-            turn("g", b + 1, 0, 0, 1)
-            turn("g", b + 1, 1, 0, 0)
-            quantise("g", b + 1, 0, 0)
-            turn("g", b + 1, 1, 0, 1)
-            scales(b + 1)
-            factor(b + 1)
-            nonzero_b1(b + 2)
-            quantise("g", b + 1, 1, 0)
-            turn("g", b + 1, 0, 1, 0)
-            row_max(b + 2)
-            turn("g", b + 1, 0, 1, 1)
+            decide(b + 1, 4)
             turn("g", b + 1, 1, 1, 0)
             quantise("g", b + 1, 0, 1)
+            decide(b + 1, 5)
             turn("g", b + 1, 1, 1, 1)
             signed_hits(b + 1)

@@ -47,6 +47,8 @@ def tile_updateonrightwithselectiveresetonleft_kernel(tc, A1_atop_B1, A2_atop_B2
         nc.vector.memset(ones[:], 1.0)
         onesb = const.tile([P, 2], BF16, name="onesb")
         nc.vector.memset(onesb[:], 1.0)
+        fill = const.tile([P, D], BF16, name="fill")
+        nc.vector.memset(fill[:], 0.0)
         junk = const.tile([P, 2 * D], F32, name="junk")
         pst = statp.tile([P, D], F32, name="pst")
         cst = statp.tile([P, D], F32, name="cst")
@@ -218,6 +220,10 @@ def tile_updateonrightwithselectiveresetonleft_kernel(tc, A1_atop_B1, A2_atop_B2
                 nc.vector.tensor_scalar(out=s[:, 10:11], in0=s[:, 9:10], scalar1=s[:, 3:4], scalar2=-1.0, op0=ALU.mult,
                                         op1=ALU.mult)
 
+        def warm(k):
+            for i in range(k):
+                nc.tensor.matmul(out=cst[:], lhsT=fill[:, 0:P], rhs=fill[:], start=True, stop=True)
+
         def dot(b, i):
             if i == 0:
                 dots[b] = smallp.tile([P, 2], F32, name="dots")
@@ -251,12 +257,12 @@ def tile_updateonrightwithselectiveresetonleft_kernel(tc, A1_atop_B1, A2_atop_B2
                 for n in range(N):
                     load_g(b, n, h)
 
-        load_a2(0, 0, halves=2)
         load_a1(0)
+        load_a2(0, 0, halves=2)
+        load_b1(0)
         load_a2(0, 1)
         load_g(0, 0, 0)
         load_g(0, 1, 0)
-        load_b1(0)
         load_a1(1)
         load_g(0, 0, 1)
         load_g(0, 1, 1)
@@ -275,45 +281,51 @@ def tile_updateonrightwithselectiveresetonleft_kernel(tc, A1_atop_B1, A2_atop_B2
             for n in range(N):
                 load_g(2, n, h)
         alloc_codes(0)
+        warm(4)
+        abs_a1(0)
         turn("a", 0, 0, 0, 0)
         turn("a", 0, 0, 0, 1)
-        abs_a1(0)
         row_max(0)
-        quantise("a", 0, 0)
-        turn("a", 0, 1, 0, 0)
-        turn("a", 0, 1, 0, 1)
+        warm(2)
+        nonzero_b1(0)
         column_sums(0, wt, 0)
         spread_max(0)
-        turn("g", 0, 0, 0, 0)
-        whole_max(0)
-        turn("g", 0, 0, 0, 1)
-        quantise("a", 0, 1)
-        hits(0)
-        turn("g", 0, 1, 0, 0)
-        turn("g", 0, 1, 0, 1)
-        column_sums(0, hit, 2)
-        nonzero_b1(0)
-        quantise("g", 0, 0, 0)
-        quantise("g", 0, 1, 0)
-        turn("g", 0, 0, 1, 0)
         column_sums(0, b1, 1)
+        quantise("a", 0, 0)
+        whole_max(0)
+        warm(2)
+        turn("a", 0, 1, 0, 0)
+        turn("a", 0, 1, 0, 1)
+        hits(0)
+        column_sums(0, hit, 2)
         partials(0)
-        turn("g", 0, 0, 1, 1)
+        turn("g", 0, 0, 0, 0)
         sum_partials(0)
         totals(0)
-        turn("g", 0, 1, 1, 0)
-        abs_a1(1)
+        quantise("a", 0, 1)
+        warm(2)
+        turn("g", 0, 0, 0, 1)
+        signed_hits(0)
         decide(0, 0)
-        quantise("g", 0, 0, 1)
+        turn("g", 0, 1, 0, 0)
+        turn("g", 0, 1, 0, 1)
+        quantise("g", 0, 0, 0)
         decide(0, 1)
         decide(0, 2)
-        row_max(1)
+        warm(2)
+        turn("g", 0, 0, 1, 0)
+        abs_a1(1)
         decide(0, 3)
-        turn("g", 0, 1, 1, 1)
-        nonzero_b1(1)
+        turn("g", 0, 0, 1, 1)
+        quantise("g", 0, 1, 0)
         decide(0, 4)
-        signed_hits(0)
+        warm(2)
+        turn("g", 0, 1, 1, 0)
+        row_max(1)
         decide(0, 5)
+        turn("g", 0, 1, 1, 1)
+        quantise("g", 0, 0, 1)
+        nonzero_b1(1)
 
         for b in range(B):
             last = b == B - 1
@@ -321,6 +333,7 @@ def tile_updateonrightwithselectiveresetonleft_kernel(tc, A1_atop_B1, A2_atop_B2
             quantise("g", b, 1, 1)
             multiply(b, 0, 1)
             column_sums(b + 1, wt, 0)
+            column_sums(b + 1, b1, 1)
             spread_max(b + 1)
             whole_max(b + 1)
             if b == 0:
@@ -340,7 +353,6 @@ def tile_updateonrightwithselectiveresetonleft_kernel(tc, A1_atop_B1, A2_atop_B2
             multiply(b, 0, 2)
             quantise("a", b + 1, 0)
             multiply(b, 0, 3)
-            column_sums(b + 1, b1, 1)
             turn("a", b + 1, 1, 0, 1)
             dot(b, 1)
             turn("g", b + 1, 0, 0, 0)

@@ -19,6 +19,7 @@ N = 2
 D = 512
 P = 128
 FLOPS = 2 * B * (2 * D) * D * (N * D)
+NZ_ON_SCALAR = (0,)
 BYTES = B * (2 * D * D * 2 + N * D * D * 2 + N * 2 * D * D * 2 + 2 * D * D * 4)
 
 
@@ -50,6 +51,7 @@ def tile_updateonrightwithselectiveresetonleft_kernel(tc, A1_atop_B1, A2_atop_B2
         fill = const.tile([P, D], BF16, name="fill")
         nc.vector.memset(fill[:], 0.0)
         junk = const.tile([P, 2 * D], F32, name="junk")
+        junkb = const.tile([P, 4 * D], BF16, name="junkb")
         pst = statp.tile([P, D], F32, name="pst")
         cst = statp.tile([P, D], F32, name="cst")
 
@@ -143,6 +145,11 @@ def tile_updateonrightwithselectiveresetonleft_kernel(tc, A1_atop_B1, A2_atop_B2
         def nonzero_b1(b):
             if b >= B:
                 return
+            if b in NZ_ON_SCALAR:
+                part[b] = smallp.tile([P, 6], F32, name="part")
+                nc.vector.memset(part[b][:, 5:6], 0.0)
+                nc.scalar.activation(out=junkb[:], in_=b1[b][:], func=ACTF.Abs, accum_out=part[b][:, 4:5])
+                return
             nc.vector.tensor_scalar(out=b1[b][:], in0=b1[b][:], scalar1=0.0, scalar2=None, op0=ALU.not_equal)
 
         def row_max(b):
@@ -153,7 +160,7 @@ def tile_updateonrightwithselectiveresetonleft_kernel(tc, A1_atop_B1, A2_atop_B2
                                     op1=ALU.max, accum_out=sc[b][:, 11:12])
 
         def column_sums(b, x, i):
-            if b >= B:
+            if b >= B or (x is b1 and b in NZ_ON_SCALAR):
                 return
             lo = 32 * b + 2 * i
             for c in range(16):
@@ -163,13 +170,13 @@ def tile_updateonrightwithselectiveresetonleft_kernel(tc, A1_atop_B1, A2_atop_B2
         def spread_max(b):
             if b >= B:
                 return
-            nc.tensor.matmul(out=pst[:, P:2 * P], lhsT=sc[b][:, 11:12].to_broadcast([P, P]), rhs=ident[:], start=True,
+            nc.tensor.matmul(out=cst[:, P:2 * P], lhsT=sc[b][:, 11:12].to_broadcast([P, P]), rhs=ident[:], start=True,
                              stop=True)
 
         def whole_max(b):
             if b >= B:
                 return
-            nc.vector.tensor_reduce(out=sc[b][:, 0:1], in_=pst[:, P:2 * P], axis=AX.X, op=ALU.max)
+            nc.vector.tensor_reduce(out=sc[b][:, 0:1], in_=cst[:, P:2 * P], axis=AX.X, op=ALU.max)
 
         def hits(b):
             if b >= B:
@@ -184,8 +191,11 @@ def tile_updateonrightwithselectiveresetonleft_kernel(tc, A1_atop_B1, A2_atop_B2
         def partials(b):
             if b >= B:
                 return
-            part[b] = smallp.tile([P, 6], F32, name="part")
-            nc.scalar.copy(out=part[b][:], in_=pst[:, 32 * b:32 * b + 6])
+            if b in NZ_ON_SCALAR:
+                nc.scalar.copy(out=part[b][:, 0:4], in_=pst[:, 32 * b:32 * b + 4])
+            else:
+                part[b] = smallp.tile([P, 6], F32, name="part")
+                nc.scalar.copy(out=part[b][:], in_=pst[:, 32 * b:32 * b + 6])
 
         def sum_partials(b):
             if b >= B:
@@ -203,7 +213,7 @@ def tile_updateonrightwithselectiveresetonleft_kernel(tc, A1_atop_B1, A2_atop_B2
                 return
             s, t_ = sc[b], total[b]
             if step == 0:
-                nc.vector.tensor_scalar(out=s[:, 2:3], in0=t_[:, 2:3], scalar1=0.0, scalar2=t_[:, 0:1],
+                nc.vector.tensor_scalar(out=s[:, 2:3], in0=t_[:, 4:5], scalar1=0.0, scalar2=t_[:, 0:1],
                                         op0=ALU.is_equal, op1=ALU.mult)
             if step == 1:
                 nc.vector.tensor_scalar(out=s[:, 3:4], in0=s[:, 2:3], scalar1=float(D * D), scalar2=None, op0=ALU.is_gt)
@@ -212,7 +222,7 @@ def tile_updateonrightwithselectiveresetonleft_kernel(tc, A1_atop_B1, A2_atop_B2
                 nc.vector.tensor_scalar(out=s[:, 4:5], in0=s[:, 3:4], scalar1=s[:, 0:1], scalar2=1.0, op0=ALU.mult,
                                         op1=ALU.max)
             if step == 3:
-                nc.vector.tensor_scalar(out=s[:, 5:6], in0=s[:, 4:5], scalar1=s[:, 4:5], scalar2=t_[:, 4:5],
+                nc.vector.tensor_scalar(out=s[:, 5:6], in0=s[:, 4:5], scalar1=s[:, 4:5], scalar2=t_[:, 2:3],
                                         op0=ALU.mult, op1=ALU.mult)
             if step == 4:
                 nc.vector.reciprocal(out=s[:, 8:10], in_=s[:, 4:6])
@@ -290,14 +300,14 @@ def tile_updateonrightwithselectiveresetonleft_kernel(tc, A1_atop_B1, A2_atop_B2
         nonzero_b1(0)
         column_sums(0, wt, 0)
         spread_max(0)
-        column_sums(0, b1, 1)
+        column_sums(0, b1, 2)
         quantise("a", 0, 0)
         whole_max(0)
         warm(2)
         turn("a", 0, 1, 0, 0)
         turn("a", 0, 1, 0, 1)
         hits(0)
-        column_sums(0, hit, 2)
+        column_sums(0, hit, 1)
         partials(0)
         turn("g", 0, 0, 0, 0)
         sum_partials(0)
@@ -327,15 +337,14 @@ def tile_updateonrightwithselectiveresetonleft_kernel(tc, A1_atop_B1, A2_atop_B2
         quantise("g", 0, 0, 1)
         nonzero_b1(1)
 
-        for b in range(B):
-            last = b == B - 1
+        for b in range(B - 2):
+            e = b + 1
             multiply(b, 0, 0)
             quantise("g", b, 1, 1)
             multiply(b, 0, 1)
-            column_sums(b + 1, wt, 0)
-            column_sums(b + 1, b1, 1)
-            spread_max(b + 1)
-            whole_max(b + 1)
+            column_sums(e, wt, 0)
+            spread_max(e)
+            whole_max(e)
             if b == 0:
                 load_a1(3)
                 load_b1(3)
@@ -344,50 +353,125 @@ def tile_updateonrightwithselectiveresetonleft_kernel(tc, A1_atop_B1, A2_atop_B2
                 for h in range(2):
                     for n in range(N):
                         load_g(3, n, h)
-            alloc_codes(b + 1)
-            turn("a", b + 1, 0, 0, 0)
+            alloc_codes(e)
+            turn("a", e, 0, 0, 0)
             dot(b, 0)
-            turn("a", b + 1, 0, 0, 1)
-            hits(b + 1)
-            turn("a", b + 1, 1, 0, 0)
+            turn("a", e, 0, 0, 1)
+            hits(e)
+            turn("a", e, 1, 0, 0)
             multiply(b, 0, 2)
-            quantise("a", b + 1, 0)
+            quantise("a", e, 0)
             multiply(b, 0, 3)
-            turn("a", b + 1, 1, 0, 1)
+            column_sums(e, b1, 2)
+            turn("a", e, 1, 0, 1)
             dot(b, 1)
-            turn("g", b + 1, 0, 0, 0)
-            column_sums(b + 1, hit, 2)
-            partials(b + 1)
+            turn("g", e, 0, 0, 0)
+            column_sums(e, hit, 1)
+            partials(e)
             abs_a1(b + 2)
-            turn("g", b + 1, 0, 0, 1)
-            quantise("a", b + 1, 1)
+            turn("g", e, 0, 0, 1)
+            quantise("a", e, 1)
             multiply(b, 1, 0)
             multiply(b, 1, 1)
-            sum_partials(b + 1)
-            totals(b + 1)
-            quantise("g", b + 1, 0, 0)
+            sum_partials(e)
+            totals(e)
+            quantise("g", e, 0, 0)
             nonzero_b1(b + 2)
-            decide(b + 1, 0)
-            turn("g", b + 1, 1, 0, 0)
+            decide(e, 0)
+            turn("g", e, 1, 0, 0)
             row_max(b + 2)
-            decide(b + 1, 1)
-            turn("g", b + 1, 1, 0, 1)
+            decide(e, 1)
+            turn("g", e, 1, 0, 1)
             coefficient(b)
-            turn("g", b + 1, 0, 1, 0)
-            quantise("g", b + 1, 1, 0)
-            decide(b + 1, 2)
+            turn("g", e, 0, 1, 0)
+            quantise("g", e, 1, 0)
+            decide(e, 2)
             multiply(b, 1, 2)
-            correct(b, 0, 2 * D)
-            store(b, 0, 0, 2 * D)
-            decide(b + 1, 3)
+            correct(b, 0 * 4 * D // 2, 1 * 4 * D // 2)
+            store(b, 0, 0 * 4 * D // 2, 1 * 4 * D // 2)
+            decide(e, 3)
             multiply(b, 1, 3)
-            store(b, 1, 0, 4 * D)
-            turn("g", b + 1, 0, 1, 1)
-            correct(b, 2 * D, 4 * D)
-            store(b, 0, 2 * D, 4 * D)
-            decide(b + 1, 4)
-            turn("g", b + 1, 1, 1, 0)
-            quantise("g", b + 1, 0, 1)
-            decide(b + 1, 5)
-            turn("g", b + 1, 1, 1, 1)
-            signed_hits(b + 1)
+            store(b, 1, 0 * 4 * D // 1, 1 * 4 * D // 1)
+            turn("g", e, 0, 1, 1)
+            correct(b, 1 * 4 * D // 2, 2 * 4 * D // 2)
+            store(b, 0, 1 * 4 * D // 2, 2 * 4 * D // 2)
+            decide(e, 4)
+            turn("g", e, 1, 1, 0)
+            quantise("g", e, 0, 1)
+            decide(e, 5)
+            turn("g", e, 1, 1, 1)
+            signed_hits(e)
+        b, e = B - 2, B - 1
+        multiply(b, 0, 0)
+        quantise("g", b, 1, 1)
+        multiply(b, 0, 1)
+        column_sums(e, wt, 0)
+        spread_max(e)
+        whole_max(e)
+        alloc_codes(e)
+        turn("a", e, 0, 0, 0)
+        dot(b, 0)
+        turn("a", e, 0, 0, 1)
+        hits(e)
+        turn("a", e, 1, 0, 0)
+        turn("a", e, 1, 0, 1)
+        multiply(b, 0, 2)
+        quantise("a", e, 0)
+        multiply(b, 0, 3)
+        column_sums(e, b1, 2)
+        turn("g", e, 0, 0, 0)
+        dot(b, 1)
+        turn("g", e, 0, 0, 1)
+        column_sums(e, hit, 1)
+        partials(e)
+        quantise("a", e, 1)
+        multiply(b, 1, 0)
+        turn("g", e, 1, 0, 0)
+        sum_partials(e)
+        totals(e)
+        quantise("g", e, 0, 0)
+        turn("g", e, 1, 0, 1)
+        multiply(b, 1, 1)
+        decide(e, 0)
+        quantise("g", e, 1, 0)
+        coefficient(b)
+        decide(e, 1)
+        multiply(b, 1, 2)
+        turn("g", e, 0, 1, 0)
+        decide(e, 2)
+        multiply(b, 1, 3)
+        store(b, 1, 0 * 4 * D // 1, 1 * 4 * D // 1)
+        decide(e, 3)
+        correct(b, 0 * 4 * D // 2, 1 * 4 * D // 2)
+        store(b, 0, 0 * 4 * D // 2, 1 * 4 * D // 2)
+        decide(e, 4)
+        multiply(e, 0, 0)
+        turn("g", e, 0, 1, 1)
+        signed_hits(e)
+        decide(e, 5)
+        multiply(e, 0, 1)
+        turn("g", e, 1, 1, 0)
+        quantise("g", e, 0, 1)
+        multiply(e, 0, 2)
+        turn("g", e, 1, 1, 1)
+        correct(b, 1 * 4 * D // 2, 2 * 4 * D // 2)
+        store(b, 0, 1 * 4 * D // 2, 2 * 4 * D // 2)
+        multiply(e, 0, 3)
+        quantise("g", e, 1, 1)
+        multiply(e, 1, 0)
+        multiply(e, 1, 1)
+        dot(e, 0)
+        store(e, 1, 0 * 4 * D // 2, 1 * 4 * D // 2)
+        multiply(e, 1, 2)
+        dot(e, 1)
+        multiply(e, 1, 3)
+        store(e, 1, 1 * 4 * D // 2, 2 * 4 * D // 2)
+        coefficient(e)
+        correct(e, 0 * 4 * D // 4, 1 * 4 * D // 4)
+        store(e, 0, 0 * 4 * D // 4, 1 * 4 * D // 4)
+        correct(e, 1 * 4 * D // 4, 2 * 4 * D // 4)
+        store(e, 0, 1 * 4 * D // 4, 2 * 4 * D // 4)
+        correct(e, 2 * 4 * D // 4, 3 * 4 * D // 4)
+        store(e, 0, 2 * 4 * D // 4, 3 * 4 * D // 4)
+        correct(e, 3 * 4 * D // 4, 4 * 4 * D // 4)
+        store(e, 0, 3 * 4 * D // 4, 4 * 4 * D // 4)

@@ -37,8 +37,7 @@ def tile_updateonrightwithselectiveresetonleft_kernel(tc, A1_atop_B1, A2_atop_B2
         codep = ctx.enter_context(tc.tile_pool(name="codep", bufs=2))
         op = ctx.enter_context(tc.tile_pool(name="op", bufs=5))
         smallp = ctx.enter_context(tc.tile_pool(name="smallp", bufs=3))
-        xtp = ctx.enter_context(tc.psum_pool(name="xtp", bufs=3))
-        accp = ctx.enter_context(tc.psum_pool(name="accp", bufs=3))
+        bankp = ctx.enter_context(tc.psum_pool(name="bankp", bufs=6))
         statp = ctx.enter_context(tc.psum_pool(name="statp", bufs=1))
         ctx.enter_context(tc.manual_schedule())
 
@@ -50,7 +49,7 @@ def tile_updateonrightwithselectiveresetonleft_kernel(tc, A1_atop_B1, A2_atop_B2
         nc.vector.memset(onesb[:], 1.0)
         fill = const.tile([P, D], BF16, name="fill")
         nc.vector.memset(fill[:], 0.0)
-        junk = const.tile([P, 2 * D], F32, name="junk")
+        junk = [const.tile([P, 2 * D], F32, name="junk" + str(i)) for i in range(2)]
         junkb = const.tile([P, 4 * D], BF16, name="junkb")
         pst = statp.tile([P, D], F32, name="pst")
         cst = statp.tile([P, D], F32, name="cst")
@@ -96,16 +95,17 @@ def tile_updateonrightwithselectiveresetonleft_kernel(tc, A1_atop_B1, A2_atop_B2
             src = (a2[b, n] if kind == "a" else g[b, n, h])[:].bitcast(F32)
             if i == 0:
                 grp[kind, b, n, h] = grpp.tile([P, 4 * D], BF16, name="grp", align_bytes=64)
-            xt = xtp.tile([P, 4, P], F32, name="xt")
+            bank = bankp.tile([P, D], F32, name="bank")
+            xt = bank[:].rearrange("p (s r) -> p s r", s=4)
             for s in range(4):
                 lo = i * 512 + s * P
                 nc.tensor.transpose(xt[:, s, :], src[:, lo:lo + P], ident[:])
             half = grp[kind, b, n, h][:].bitcast(F32)[:, i * 512:(i + 1) * 512]
             if kind == "a":
-                nc.scalar.copy(out=half.rearrange("q (r s) -> q r s", s=4), in_=xt[:].rearrange("q s r -> q r s"))
+                nc.scalar.copy(out=half.rearrange("q (r s) -> q r s", s=4), in_=xt.rearrange("q s r -> q r s"))
             else:
                 nc.scalar.copy(out=half.rearrange("q (t r u) -> q t r u", t=2, u=2),
-                               in_=xt[:].rearrange("q (t u) r -> q t r u", t=2, u=2))
+                               in_=xt.rearrange("q (t u) r -> q t r u", t=2, u=2))
 
         def quantise(kind, b, n, h=0):
             if b >= B:
@@ -126,7 +126,7 @@ def tile_updateonrightwithselectiveresetonleft_kernel(tc, A1_atop_B1, A2_atop_B2
             if t == 0:
                 osb[b, h] = op.tile([P, 4 * D], F32, name="osb")
             scale = sc[b][:, 8:9] if h == 0 else sc[b][:, 1:2]
-            acc = accp.tile([P, D], F32, name="acc")
+            acc = bankp.tile([P, D], F32, name="bank")
             for n in range(N):
                 lo = n * 2 * D + h * D + t * P
                 nc.tensor.matmul_mx(out=acc[:], lhsT=gc[:, lo:lo + P].bitcast(E5), lhsT_scale=gs[:, lo:lo + P],
@@ -232,13 +232,14 @@ def tile_updateonrightwithselectiveresetonleft_kernel(tc, A1_atop_B1, A2_atop_B2
 
         def warm(k):
             for i in range(k):
-                nc.tensor.matmul(out=cst[:], lhsT=fill[:, 0:P], rhs=fill[:], start=True, stop=True)
+                acc = bankp.tile([P, D], F32, name="bank")
+                nc.tensor.matmul(out=acc[:], lhsT=fill[:, 0:P], rhs=fill[:], start=True, stop=True)
 
         def dot(b, i):
             if i == 0:
                 dots[b] = smallp.tile([P, 2], F32, name="dots")
             cols = slice(i * 2 * D, (i + 1) * 2 * D)
-            nc.vector.scalar_tensor_tensor(out=junk[:], in0=osb[b, 0][:, cols], scalar=1.0, in1=a1[b][:, cols],
+            nc.vector.scalar_tensor_tensor(out=junk[i][:], in0=osb[b, 0][:, cols], scalar=1.0, in1=a1[b][:, cols],
                                            op0=ALU.mult, op1=ALU.mult, accum_out=dots[b][:, i:i + 1])
 
         def coefficient(b):

@@ -56,7 +56,7 @@ def tile_updateonrightwithselectiveresetonleft_kernel(tc, A1_atop_B1, A2_atop_B2
 
         a1, b1, a2, g = {}, {}, {}, {}
         wt, hit, sc, dots, part, total = {}, {}, {}, {}, {}, {}
-        grp, codes, osb = {}, {}, {}
+        grp, codes, osb, spread, kept = {}, {}, {}, {}, {}
 
         def load_a1(b):
             a1[b] = a1p.tile([P, 4 * D], BF16, name="a1")
@@ -125,7 +125,7 @@ def tile_updateonrightwithselectiveresetonleft_kernel(tc, A1_atop_B1, A2_atop_B2
             gc, gs, ac, as_ = codes[b]
             if t == 0:
                 osb[b, h] = op.tile([P, 4 * D], F32, name="osb")
-            scale = sc[b][:, 8:9] if h == 0 else sc[b][:, 1:2]
+            scale = sc[b][:, 8:9] if h == 0 else kept[b][:, 0:1]
             acc = bankp.tile([P, D], F32, name="bank")
             for n in range(N):
                 lo = n * 2 * D + h * D + t * P
@@ -156,6 +156,7 @@ def tile_updateonrightwithselectiveresetonleft_kernel(tc, A1_atop_B1, A2_atop_B2
             if b >= B:
                 return
             sc[b] = smallp.tile([P, 12], F32, name="sc")
+            kept[b] = smallp.tile([P, 16], F32, name="kept")
             nc.vector.tensor_scalar(out=hit[b][:], in0=wt[b][:], scalar1=1.0, scalar2=None, op0=ALU.mult,
                                     op1=ALU.max, accum_out=sc[b][:, 11:12])
 
@@ -170,13 +171,14 @@ def tile_updateonrightwithselectiveresetonleft_kernel(tc, A1_atop_B1, A2_atop_B2
         def spread_max(b):
             if b >= B:
                 return
-            nc.tensor.matmul(out=cst[:, P:2 * P], lhsT=sc[b][:, 11:12].to_broadcast([P, P]), rhs=ident[:], start=True,
+            spread[b] = bankp.tile([P, D], F32, name="bank")
+            nc.tensor.matmul(out=spread[b][:, 0:P], lhsT=sc[b][:, 11:12].to_broadcast([P, P]), rhs=ident[:], start=True,
                              stop=True)
 
         def whole_max(b):
             if b >= B:
                 return
-            nc.vector.tensor_reduce(out=sc[b][:, 0:1], in_=cst[:, P:2 * P], axis=AX.X, op=ALU.max)
+            nc.vector.tensor_reduce(out=sc[b][:, 0:1], in_=spread[b][:, 0:P], axis=AX.X, op=ALU.max)
 
         def hits(b):
             if b >= B:
@@ -217,7 +219,7 @@ def tile_updateonrightwithselectiveresetonleft_kernel(tc, A1_atop_B1, A2_atop_B2
                                         op0=ALU.is_equal, op1=ALU.mult)
             if step == 1:
                 nc.vector.tensor_scalar(out=s[:, 3:4], in0=s[:, 2:3], scalar1=float(D * D), scalar2=None, op0=ALU.is_gt)
-                nc.vector.tensor_scalar(out=s[:, 1:2], in0=s[:, 2:3], scalar1=float(D * D), scalar2=None, op0=ALU.is_le)
+                nc.gpsimd.tensor_scalar(out=kept[b][:, 0:1], in0=s[:, 2:3], scalar1=float(D * D), scalar2=None, op0=ALU.is_le)
             if step == 2:
                 nc.vector.tensor_scalar(out=s[:, 4:5], in0=s[:, 3:4], scalar1=s[:, 0:1], scalar2=1.0, op0=ALU.mult,
                                         op1=ALU.max)
@@ -227,7 +229,7 @@ def tile_updateonrightwithselectiveresetonleft_kernel(tc, A1_atop_B1, A2_atop_B2
             if step == 4:
                 nc.vector.reciprocal(out=s[:, 8:10], in_=s[:, 4:6])
             if step == 5:
-                nc.vector.tensor_scalar(out=s[:, 10:11], in0=s[:, 9:10], scalar1=s[:, 3:4], scalar2=-1.0, op0=ALU.mult,
+                nc.gpsimd.tensor_scalar(out=kept[b][:, 8:9], in0=s[:, 9:10], scalar1=s[:, 3:4], scalar2=-1.0, op0=ALU.mult,
                                         op1=ALU.mult)
 
         def warm(k):
@@ -244,7 +246,7 @@ def tile_updateonrightwithselectiveresetonleft_kernel(tc, A1_atop_B1, A2_atop_B2
 
         def coefficient(b):
             for i in range(2):
-                nc.tensor.matmul(out=cst[:, b:b + 1], lhsT=sc[b][:, 10:11].to_broadcast([P, P]),
+                nc.tensor.matmul(out=cst[:, b:b + 1], lhsT=kept[b][:, 8:9].to_broadcast([P, P]),
                                  rhs=dots[b][:, i:i + 1], start=(i == 0), stop=(i == 1))
 
         def correct(b, lo, hi):

@@ -19,7 +19,7 @@ N = 2
 D = 512
 P = 128
 FLOPS = 2 * B * (2 * D) * D * (N * D)
-NZ_ON_SCALAR = (0,)
+NZ_ON_SCALAR = ()
 BYTES = B * (2 * D * D * 2 + N * D * D * 2 + N * 2 * D * D * 2 + 2 * D * D * 4)
 
 
@@ -300,28 +300,28 @@ def tile_updateonrightwithselectiveresetonleft_kernel(tc, A1_atop_B1, A2_atop_B2
         turn("a", 0, 0, 0, 1)
         row_max(0)
         warm(2)
-        nonzero_b1(0)
         column_sums(0, wt, 0)
         spread_max(0)
-        column_sums(0, b1, 2)
+        nonzero_b1(0)
         quantise("a", 0, 0)
         whole_max(0)
         warm(2)
+        column_sums(0, b1, 2)
         turn("a", 0, 1, 0, 0)
         turn("a", 0, 1, 0, 1)
         hits(0)
+        turn("g", 0, 0, 0, 0)
         column_sums(0, hit, 1)
         partials(0)
-        turn("g", 0, 0, 0, 0)
+        signed_hits(0)
+        warm(2)
+        turn("g", 0, 0, 0, 1)
         sum_partials(0)
         totals(0)
         quantise("a", 0, 1)
-        warm(2)
-        turn("g", 0, 0, 0, 1)
-        signed_hits(0)
-        decide(0, 0)
         turn("g", 0, 1, 0, 0)
         turn("g", 0, 1, 0, 1)
+        decide(0, 0)
         quantise("g", 0, 0, 0)
         decide(0, 1)
         decide(0, 2)

@@ -455,20 +455,22 @@ def tile_updateonrightwithselectiveresetonleft_kernel(tc, A1_atop_B1, A2_atop_B2
         multiply(e, 0, 1)
         turn("g", e, 1, 1, 0)
         quantise("g", e, 0, 1)
-        multiply(e, 0, 2)
         turn("g", e, 1, 1, 1)
         correct(b, 1 * 4 * D // 2, 2 * 4 * D // 2)
         store(b, 0, 1 * 4 * D // 2, 2 * 4 * D // 2)
-        multiply(e, 0, 3)
         quantise("g", e, 1, 1)
+        multiply(e, 0, 2)
+        multiply(e, 0, 3)
         multiply(e, 1, 0)
-        multiply(e, 1, 1)
+        store(e, 1, 0 * 4 * D // 4, 1 * 4 * D // 4)
         dot(e, 0)
-        store(e, 1, 0 * 4 * D // 2, 1 * 4 * D // 2)
-        multiply(e, 1, 2)
+        multiply(e, 1, 1)
+        store(e, 1, 1 * 4 * D // 4, 2 * 4 * D // 4)
         dot(e, 1)
+        multiply(e, 1, 2)
+        store(e, 1, 2 * 4 * D // 4, 3 * 4 * D // 4)
         multiply(e, 1, 3)
-        store(e, 1, 1 * 4 * D // 2, 2 * 4 * D // 2)
+        store(e, 1, 3 * 4 * D // 4, 4 * 4 * D // 4)
         coefficient(e)
         correct(e, 0 * 4 * D // 4, 1 * 4 * D // 4)
         store(e, 0, 0 * 4 * D // 4, 1 * 4 * D // 4)

@@ -19,7 +19,7 @@ N = 2
 D = 512
 P = 128
 FLOPS = 2 * B * (2 * D) * D * (N * D)
-NZ_ON_SCALAR = ()
+VETO = -float(2 ** 40)
 BYTES = B * (2 * D * D * 2 + N * D * D * 2 + N * 2 * D * D * 2 + 2 * D * D * 4)
 
 
@@ -47,10 +47,11 @@ def tile_updateonrightwithselectiveresetonleft_kernel(tc, A1_atop_B1, A2_atop_B2
         nc.vector.memset(ones[:], 1.0)
         onesb = const.tile([P, 2], BF16, name="onesb")
         nc.vector.memset(onesb[:], 1.0)
+        veto = const.tile([P, 2], BF16, name="veto")
+        nc.vector.memset(veto[:], VETO)
         fill = const.tile([P, D], BF16, name="fill")
         nc.vector.memset(fill[:], 0.0)
-        junk = [const.tile([P, 2 * D], F32, name="junk" + str(i)) for i in range(2)]
-        junkb = const.tile([P, 4 * D], BF16, name="junkb")
+        junk = const.tile([P, 4 * D], F32, name="junk")
         pst = statp.tile([P, D], F32, name="pst")
         cst = statp.tile([P, D], F32, name="cst")
 
@@ -145,28 +146,39 @@ def tile_updateonrightwithselectiveresetonleft_kernel(tc, A1_atop_B1, A2_atop_B2
         def nonzero_b1(b):
             if b >= B:
                 return
-            if b in NZ_ON_SCALAR:
-                part[b] = smallp.tile([P, 6], F32, name="part")
-                nc.vector.memset(part[b][:, 5:6], 0.0)
-                nc.scalar.activation(out=junkb[:], in_=b1[b][:], func=ACTF.Abs, accum_out=part[b][:, 4:5])
-                return
             nc.vector.tensor_scalar(out=b1[b][:], in0=b1[b][:], scalar1=0.0, scalar2=None, op0=ALU.not_equal)
 
-        def row_max(b):
+        def row_max(b, step):
             if b >= B:
                 return
-            sc[b] = smallp.tile([P, 12], F32, name="sc")
-            kept[b] = smallp.tile([P, 16], F32, name="kept")
-            nc.vector.tensor_scalar(out=hit[b][:], in0=wt[b][:], scalar1=1.0, scalar2=None, op0=ALU.mult,
-                                    op1=ALU.max, accum_out=sc[b][:, 11:12])
+            if step == 0:
+                sc[b] = smallp.tile([P, 12], F32, name="sc")
+                kept[b] = smallp.tile([P, 16], F32, name="kept")
+            src = wt[b] if step == 0 else hit[b]
+            lo = (0, 0, 2 * D, 3 * D)[step]
+            width = 2 * D >> step
+            if step == 3:
+                nc.vector.tensor_reduce(out=sc[b][:, 11:12], in_=src[:, lo:lo + 2 * width], axis=AX.X, op=ALU.max)
+            else:
+                dst = (0, 2 * D, 3 * D)[step]
+                nc.vector.tensor_tensor(out=hit[b][:, dst:dst + width], in0=src[:, lo:lo + width],
+                                        in1=src[:, lo + width:lo + 2 * width], op=ALU.max)
 
-        def column_sums(b, x, i):
-            if b >= B or (x is b1 and b in NZ_ON_SCALAR):
+        def column_sums(b, i, pairs):
+            if b >= B:
                 return
             lo = 32 * b + 2 * i
-            for c in range(16):
-                nc.tensor.matmul(out=pst[:, lo:lo + 2], lhsT=x[b][:, c * P:(c + 1) * P], rhs=onesb[:], start=(c == 0),
-                                 stop=(c == 15))
+            last = (len(pairs) - 1, 15)
+            for k, (x, w) in enumerate(pairs):
+                for c in range(16):
+                    nc.tensor.matmul(out=pst[:, lo:lo + 2], lhsT=x[b][:, c * P:(c + 1) * P], rhs=w[:], start=(k == 0 and c == 0),
+                                     stop=((k, c) == last))
+
+        def sums_ab(b):
+            column_sums(b, 0, ((wt, onesb), (b1, veto)))
+
+        def sum_hits(b):
+            column_sums(b, 1, ((hit, onesb),))
 
         def spread_max(b):
             if b >= B:
@@ -178,12 +190,12 @@ def tile_updateonrightwithselectiveresetonleft_kernel(tc, A1_atop_B1, A2_atop_B2
         def whole_max(b):
             if b >= B:
                 return
-            nc.vector.tensor_reduce(out=sc[b][:, 0:1], in_=spread[b][:, 0:P], axis=AX.X, op=ALU.max)
+            nc.vector.tensor_reduce(out=sc[b][:, 4:5], in_=spread[b][:, 0:P], axis=AX.X, op=ALU.max)
 
         def hits(b):
             if b >= B:
                 return
-            nc.vector.tensor_scalar(out=hit[b][:], in0=wt[b][:], scalar1=sc[b][:, 0:1], scalar2=None, op0=ALU.is_equal)
+            nc.vector.tensor_scalar(out=hit[b][:], in0=wt[b][:], scalar1=sc[b][:, 4:5], scalar2=None, op0=ALU.is_equal)
 
         def signed_hits(b):
             if b >= B:
@@ -193,43 +205,37 @@ def tile_updateonrightwithselectiveresetonleft_kernel(tc, A1_atop_B1, A2_atop_B2
         def partials(b):
             if b >= B:
                 return
-            if b in NZ_ON_SCALAR:
-                nc.scalar.copy(out=part[b][:, 0:4], in_=pst[:, 32 * b:32 * b + 4])
-            else:
-                part[b] = smallp.tile([P, 6], F32, name="part")
-                nc.scalar.copy(out=part[b][:], in_=pst[:, 32 * b:32 * b + 6])
+            part[b] = smallp.tile([P, 4], F32, name="part")
+            nc.scalar.copy(out=part[b][:], in_=pst[:, 32 * b:32 * b + 4])
 
         def sum_partials(b):
             if b >= B:
                 return
-            nc.tensor.matmul(out=pst[:, 32 * b + 8:32 * b + 14], lhsT=ones[:], rhs=part[b][:], start=True, stop=True)
+            nc.tensor.matmul(out=pst[:, 32 * b + 8:32 * b + 12], lhsT=ones[:], rhs=part[b][:], start=True, stop=True)
 
         def totals(b):
             if b >= B:
                 return
-            total[b] = smallp.tile([P, 6], F32, name="total")
-            nc.scalar.copy(out=total[b][:], in_=pst[:, 32 * b + 8:32 * b + 14])
+            total[b] = smallp.tile([P, 4], F32, name="total")
+            nc.scalar.copy(out=total[b][:], in_=pst[:, 32 * b + 8:32 * b + 12])
 
         def decide(b, step):
             if b >= B:
                 return
-            s, t_ = sc[b], total[b]
+            s, t_, k_ = sc[b], total[b], kept[b]
             if step == 0:
-                nc.vector.tensor_scalar(out=s[:, 2:3], in0=t_[:, 4:5], scalar1=0.0, scalar2=t_[:, 0:1],
-                                        op0=ALU.is_equal, op1=ALU.mult)
+                nc.vector.tensor_scalar(out=s[:, 3:4], in0=t_[:, 0:1], scalar1=float(D * D), scalar2=None, op0=ALU.is_gt)
+                nc.gpsimd.tensor_scalar(out=k_[:, 0:1], in0=t_[:, 0:1], scalar1=float(D * D), scalar2=None, op0=ALU.is_le)
             if step == 1:
-                nc.vector.tensor_scalar(out=s[:, 3:4], in0=s[:, 2:3], scalar1=float(D * D), scalar2=None, op0=ALU.is_gt)
-                nc.gpsimd.tensor_scalar(out=kept[b][:, 0:1], in0=s[:, 2:3], scalar1=float(D * D), scalar2=None, op0=ALU.is_le)
-            if step == 2:
-                nc.vector.tensor_scalar(out=s[:, 4:5], in0=s[:, 3:4], scalar1=s[:, 0:1], scalar2=1.0, op0=ALU.mult,
+                nc.vector.tensor_scalar(out=s[:, 6:7], in0=s[:, 3:4], scalar1=s[:, 4:5], scalar2=1.0, op0=ALU.mult,
                                         op1=ALU.max)
-            if step == 3:
-                nc.vector.tensor_scalar(out=s[:, 5:6], in0=s[:, 4:5], scalar1=s[:, 4:5], scalar2=t_[:, 2:3],
+            if step == 2:
+                nc.vector.tensor_scalar(out=s[:, 7:8], in0=s[:, 6:7], scalar1=s[:, 6:7], scalar2=t_[:, 2:3],
                                         op0=ALU.mult, op1=ALU.mult)
+            if step == 3:
+                nc.vector.reciprocal(out=s[:, 8:10], in_=s[:, 6:8])
             if step == 4:
-                nc.vector.reciprocal(out=s[:, 8:10], in_=s[:, 4:6])
-            if step == 5:
-                nc.gpsimd.tensor_scalar(out=kept[b][:, 8:9], in0=s[:, 9:10], scalar1=s[:, 3:4], scalar2=-1.0, op0=ALU.mult,
+                nc.gpsimd.tensor_scalar(out=k_[:, 8:9], in0=s[:, 9:10], scalar1=s[:, 3:4], scalar2=-1.0, op0=ALU.mult,
                                         op1=ALU.mult)
 
         def warm(k):
@@ -237,23 +243,27 @@ def tile_updateonrightwithselectiveresetonleft_kernel(tc, A1_atop_B1, A2_atop_B2
                 acc = bankp.tile([P, D], F32, name="bank")
                 nc.tensor.matmul(out=acc[:], lhsT=fill[:, 0:P], rhs=fill[:], start=True, stop=True)
 
-        def dot(b, i):
+        def dot(b, i=0, parts=1):
             if i == 0:
                 dots[b] = smallp.tile([P, 2], F32, name="dots")
-            cols = slice(i * 2 * D, (i + 1) * 2 * D)
-            nc.vector.scalar_tensor_tensor(out=junk[i][:], in0=osb[b, 0][:, cols], scalar=1.0, in1=a1[b][:, cols],
+            cols = slice(i * 4 * D // parts, (i + 1) * 4 * D // parts)
+            nc.vector.scalar_tensor_tensor(out=junk[:, cols], in0=osb[b, 0][:, cols], scalar=1.0, in1=a1[b][:, cols],
                                            op0=ALU.mult, op1=ALU.mult, accum_out=dots[b][:, i:i + 1])
 
-        def coefficient(b):
-            for i in range(2):
-                nc.tensor.matmul(out=cst[:, b:b + 1], lhsT=kept[b][:, 8:9].to_broadcast([P, P]),
-                                 rhs=dots[b][:, i:i + 1], start=(i == 0), stop=(i == 1))
+        def coefficient(b, parts=1):
+            for i in range(parts):
+                nc.tensor.matmul(out=cst[:, b:b + 1], lhsT=kept[b][:, 8:9].to_broadcast([P, P]), rhs=dots[b][:, i:i + 1],
+                                 start=(i == 0), stop=(i == parts - 1))
 
-        def correct(b, lo, hi):
+        def correct(b, i, parts):
+            if b < 0:
+                return
+            lo, hi = i * 4 * D // parts, (i + 1) * 4 * D // parts
             cols = slice(lo, hi)
             nc.vector.scalar_tensor_tensor(out=osb[b, 0][:, cols], in0=wt[b][:, cols],
                                            scalar=cst[:, b:b + 1], in1=osb[b, 0][:, cols],
                                            op0=ALU.mult, op1=ALU.add)
+            store(b, 0, lo, hi)
 
         def store(b, h, lo, hi):
             nc.sync.dma_start(out=out[b, 0, h * D:(h + 1) * D, :].rearrange("(p t) k -> p (t k)", p=P, t=4)[:, lo:hi],
@@ -272,84 +282,84 @@ def tile_updateonrightwithselectiveresetonleft_kernel(tc, A1_atop_B1, A2_atop_B2
 
         load_a1(0)
         load_a2(0, 0, halves=2)
-        load_b1(0)
+        load_a1(1)
         load_a2(0, 1)
+        load_b1(0)
         load_g(0, 0, 0)
         load_g(0, 1, 0)
-        load_a1(1)
         load_g(0, 0, 1)
         load_g(0, 1, 1)
         load_b1(1)
         load_a2(1, 0)
         load_a2(1, 1)
+        load_a1(2)
         load_g(1, 0, 0)
         load_g(1, 1, 0)
-        load_a1(2)
         load_b1(2)
         load_g(1, 0, 1)
         load_g(1, 1, 1)
         load_a2(2, 0)
         load_a2(2, 1)
-        for h in range(2):
-            for n in range(N):
-                load_g(2, n, h)
+        load_a1(3)
+        load_g(2, 0, 0)
+        load_g(2, 1, 0)
+        load_g(2, 0, 1)
+        load_g(2, 1, 1)
         alloc_codes(0)
         warm(4)
         abs_a1(0)
         turn("a", 0, 0, 0, 0)
         turn("a", 0, 0, 0, 1)
-        row_max(0)
+        row_max(0, 0)
+        row_max(0, 1)
+        abs_a1(1)
+        row_max(0, 2)
         warm(2)
-        column_sums(0, wt, 0)
-        spread_max(0)
-        nonzero_b1(0)
         quantise("a", 0, 0)
-        whole_max(0)
+        row_max(0, 3)
         warm(2)
-        column_sums(0, b1, 2)
         turn("a", 0, 1, 0, 0)
         turn("a", 0, 1, 0, 1)
+        row_max(1, 0)
+        spread_max(0)
+        nonzero_b1(0)
+        whole_max(0)
+        row_max(1, 1)
         hits(0)
+        row_max(1, 2)
         turn("g", 0, 0, 0, 0)
-        column_sums(0, hit, 1)
+        turn("g", 0, 0, 0, 1)
+        sums_ab(0)
+        quantise("a", 0, 1)
+        sum_hits(0)
         partials(0)
         signed_hits(0)
-        warm(2)
-        turn("g", 0, 0, 0, 1)
-        sum_partials(0)
-        totals(0)
-        quantise("a", 0, 1)
         turn("g", 0, 1, 0, 0)
         turn("g", 0, 1, 0, 1)
-        decide(0, 0)
+        sum_partials(0)
+        totals(0)
         quantise("g", 0, 0, 0)
-        decide(0, 1)
-        decide(0, 2)
-        warm(2)
+        decide(0, 0)
         turn("g", 0, 0, 1, 0)
-        abs_a1(1)
-        decide(0, 3)
         turn("g", 0, 0, 1, 1)
         quantise("g", 0, 1, 0)
-        decide(0, 4)
-        warm(2)
+        decide(0, 1)
         turn("g", 0, 1, 1, 0)
-        row_max(1)
-        decide(0, 5)
-        turn("g", 0, 1, 1, 1)
+        decide(0, 2)
         quantise("g", 0, 0, 1)
-        nonzero_b1(1)
+        decide(0, 3)
+        decide(0, 4)
+        turn("g", 0, 1, 1, 1)
+        row_max(1, 3)
 
         for b in range(B - 2):
-            e = b + 1
+            e, f = b + 1, b + 2
             multiply(b, 0, 0)
-            quantise("g", b, 1, 1)
             multiply(b, 0, 1)
-            column_sums(e, wt, 0)
-            spread_max(e)
-            whole_max(e)
+            quantise("g", b, 1, 1)
+            correct(b - 1, 1, 2)
+            nonzero_b1(e)
             if b == 0:
-                load_a1(3)
                 load_b1(3)
                 load_a2(3, 0)
                 load_a2(3, 1)
@@ -358,125 +368,113 @@ def tile_updateonrightwithselectiveresetonleft_kernel(tc, A1_atop_B1, A2_atop_B2
                         load_g(3, n, h)
             alloc_codes(e)
             turn("a", e, 0, 0, 0)
-            dot(b, 0)
             turn("a", e, 0, 0, 1)
-            hits(e)
             turn("a", e, 1, 0, 0)
-            multiply(b, 0, 2)
+            abs_a1(f)
             quantise("a", e, 0)
+            multiply(b, 0, 2)
             multiply(b, 0, 3)
-            column_sums(e, b1, 2)
+            spread_max(e)
+            whole_max(e)
+            row_max(f, 0)
             turn("a", e, 1, 0, 1)
-            dot(b, 1)
             turn("g", e, 0, 0, 0)
-            column_sums(e, hit, 1)
-            partials(e)
-            abs_a1(b + 2)
+            hits(e)
+            dot(b)
             turn("g", e, 0, 0, 1)
-            quantise("a", e, 1)
             multiply(b, 1, 0)
             multiply(b, 1, 1)
+            sums_ab(e)
+            sum_hits(e)
+            partials(e)
+            quantise("a", e, 1)
+            signed_hits(e)
+            turn("g", e, 1, 0, 0)
+            turn("g", e, 1, 0, 1)
+            quantise("g", e, 0, 0)
+            turn("g", e, 0, 1, 0)
             sum_partials(e)
             totals(e)
-            quantise("g", e, 0, 0)
-            nonzero_b1(b + 2)
             decide(e, 0)
-            turn("g", e, 1, 0, 0)
-            row_max(b + 2)
+            row_max(f, 1)
             decide(e, 1)
-            turn("g", e, 1, 0, 1)
-            coefficient(b)
-            turn("g", e, 0, 1, 0)
             quantise("g", e, 1, 0)
             decide(e, 2)
-            multiply(b, 1, 2)
-            correct(b, 0 * 4 * D // 2, 1 * 4 * D // 2)
-            store(b, 0, 0 * 4 * D // 2, 1 * 4 * D // 2)
+            row_max(f, 2)
             decide(e, 3)
-            multiply(b, 1, 3)
-            store(b, 1, 0 * 4 * D // 1, 1 * 4 * D // 1)
-            turn("g", e, 0, 1, 1)
-            correct(b, 1 * 4 * D // 2, 2 * 4 * D // 2)
-            store(b, 0, 1 * 4 * D // 2, 2 * 4 * D // 2)
             decide(e, 4)
+            multiply(b, 1, 2)
+            multiply(b, 1, 3)
+            store(b, 1, 0, 4 * D)
+            coefficient(b)
+            turn("g", e, 0, 1, 1)
+            correct(b, 0, 2)
             turn("g", e, 1, 1, 0)
-            quantise("g", e, 0, 1)
-            decide(e, 5)
             turn("g", e, 1, 1, 1)
-            signed_hits(e)
+            quantise("g", e, 0, 1)
+            row_max(f, 3)
+
         b, e = B - 2, B - 1
         multiply(b, 0, 0)
-        quantise("g", b, 1, 1)
         multiply(b, 0, 1)
-        column_sums(e, wt, 0)
-        spread_max(e)
-        whole_max(e)
+        quantise("g", b, 1, 1)
+        correct(b - 1, 1, 2)
+        nonzero_b1(e)
         alloc_codes(e)
         turn("a", e, 0, 0, 0)
-        dot(b, 0)
         turn("a", e, 0, 0, 1)
-        hits(e)
         turn("a", e, 1, 0, 0)
-        turn("a", e, 1, 0, 1)
-        multiply(b, 0, 2)
         quantise("a", e, 0)
+        multiply(b, 0, 2)
         multiply(b, 0, 3)
-        column_sums(e, b1, 2)
+        spread_max(e)
+        whole_max(e)
+        turn("a", e, 1, 0, 1)
+        hits(e)
         turn("g", e, 0, 0, 0)
-        dot(b, 1)
         turn("g", e, 0, 0, 1)
-        column_sums(e, hit, 1)
+        dot(b)
+        multiply(b, 1, 0)
+        multiply(b, 1, 1)
+        sums_ab(e)
+        sum_hits(e)
         partials(e)
         quantise("a", e, 1)
-        multiply(b, 1, 0)
-        turn("g", e, 1, 0, 0)
+        signed_hits(e)
         sum_partials(e)
         totals(e)
-        quantise("g", e, 0, 0)
-        turn("g", e, 1, 0, 1)
-        multiply(b, 1, 1)
         decide(e, 0)
-        quantise("g", e, 1, 0)
-        coefficient(b)
+        turn("g", e, 1, 0, 0)
+        turn("g", e, 1, 0, 1)
+        quantise("g", e, 0, 0)
         decide(e, 1)
-        multiply(b, 1, 2)
-        turn("g", e, 0, 1, 0)
+        quantise("g", e, 1, 0)
         decide(e, 2)
+        multiply(b, 1, 2)
         multiply(b, 1, 3)
-        store(b, 1, 0 * 4 * D // 1, 1 * 4 * D // 1)
+        store(b, 1, 0, 4 * D)
+        turn("g", e, 0, 1, 0)
+        coefficient(b)
         decide(e, 3)
-        correct(b, 0 * 4 * D // 2, 1 * 4 * D // 2)
-        store(b, 0, 0 * 4 * D // 2, 1 * 4 * D // 2)
         decide(e, 4)
-        multiply(e, 0, 0)
         turn("g", e, 0, 1, 1)
-        signed_hits(e)
-        decide(e, 5)
+        correct(b, 0, 2)
+        multiply(e, 0, 0)
         multiply(e, 0, 1)
         turn("g", e, 1, 1, 0)
-        quantise("g", e, 0, 1)
         turn("g", e, 1, 1, 1)
-        correct(b, 1 * 4 * D // 2, 2 * 4 * D // 2)
-        store(b, 0, 1 * 4 * D // 2, 2 * 4 * D // 2)
-        quantise("g", e, 1, 1)
+        quantise("g", e, 0, 1)
+        correct(b, 1, 2)
         multiply(e, 0, 2)
         multiply(e, 0, 3)
+        quantise("g", e, 1, 1)
+        dot(e, 0, 2)
         multiply(e, 1, 0)
-        store(e, 1, 0 * 4 * D // 4, 1 * 4 * D // 4)
-        dot(e, 0)
-        multiply(e, 1, 1)
-        store(e, 1, 1 * 4 * D // 4, 2 * 4 * D // 4)
-        dot(e, 1)
-        multiply(e, 1, 2)
-        store(e, 1, 2 * 4 * D // 4, 3 * 4 * D // 4)
-        multiply(e, 1, 3)
-        store(e, 1, 3 * 4 * D // 4, 4 * 4 * D // 4)
-        coefficient(e)
-        correct(e, 0 * 4 * D // 4, 1 * 4 * D // 4)
-        store(e, 0, 0 * 4 * D // 4, 1 * 4 * D // 4)
-        correct(e, 1 * 4 * D // 4, 2 * 4 * D // 4)
-        store(e, 0, 1 * 4 * D // 4, 2 * 4 * D // 4)
-        correct(e, 2 * 4 * D // 4, 3 * 4 * D // 4)
-        store(e, 0, 2 * 4 * D // 4, 3 * 4 * D // 4)
-        correct(e, 3 * 4 * D // 4, 4 * 4 * D // 4)
-        store(e, 0, 3 * 4 * D // 4, 4 * 4 * D // 4)
+        store(e, 1, 0, D)
+        dot(e, 1, 2)
+        for t in range(1, 4):
+            multiply(e, 1, t)
+            store(e, 1, t * D, (t + 1) * D)
+        coefficient(e, 2)
+        for i in range(4):
+            correct(e, i, 4)

@@ -19,6 +19,7 @@ N = 2
 D = 512
 P = 128
 FLOPS = 2 * B * (2 * D) * D * (N * D)
+SUM_COLS = 32
 VETO = -float(2 ** 40)
 BYTES = B * (2 * D * D * 2 + N * D * D * 2 + N * 2 * D * D * 2 + 2 * D * D * 4)
 
@@ -28,14 +29,14 @@ def tile_updateonrightwithselectiveresetonleft_kernel(tc, A1_atop_B1, A2_atop_B2
     with ExitStack() as ctx:
         const = ctx.enter_context(tc.tile_pool(name="const", bufs=1))
         a1p = ctx.enter_context(tc.tile_pool(name="a1p", bufs=4))
-        b1p = ctx.enter_context(tc.tile_pool(name="b1p", bufs=3))
-        a2p = ctx.enter_context(tc.tile_pool(name="a2p", bufs=6))
-        gp = ctx.enter_context(tc.tile_pool(name="gp", bufs=12))
+        b1p = ctx.enter_context(tc.tile_pool(name="b1p", bufs=2))
+        a2p = ctx.enter_context(tc.tile_pool(name="a2p", bufs=4))
+        gp = ctx.enter_context(tc.tile_pool(name="gp", bufs=8))
         wtp = ctx.enter_context(tc.tile_pool(name="wtp", bufs=3))
         hitp = ctx.enter_context(tc.tile_pool(name="hitp", bufs=2))
         grpp = ctx.enter_context(tc.tile_pool(name="grpp", bufs=6))
         codep = ctx.enter_context(tc.tile_pool(name="codep", bufs=2))
-        op = ctx.enter_context(tc.tile_pool(name="op", bufs=5))
+        op = ctx.enter_context(tc.tile_pool(name="op", bufs=8))
         smallp = ctx.enter_context(tc.tile_pool(name="smallp", bufs=3))
         bankp = ctx.enter_context(tc.psum_pool(name="bankp", bufs=6))
         statp = ctx.enter_context(tc.psum_pool(name="statp", bufs=1))
@@ -45,11 +46,11 @@ def tile_updateonrightwithselectiveresetonleft_kernel(tc, A1_atop_B1, A2_atop_B2
         make_identity(nc, ident[:])
         ones = const.tile([P, P], F32, name="ones")
         nc.vector.memset(ones[:], 1.0)
-        onesb = const.tile([P, 2], BF16, name="onesb")
+        onesb = const.tile([P, SUM_COLS], BF16, name="onesb")
         nc.vector.memset(onesb[:], 1.0)
-        veto = const.tile([P, 2], BF16, name="veto")
+        veto = const.tile([P, SUM_COLS], BF16, name="veto")
         nc.vector.memset(veto[:], VETO)
-        fill = const.tile([P, D], BF16, name="fill")
+        fill = const.tile([P, P], F32, name="fill")
         nc.vector.memset(fill[:], 0.0)
         junk = const.tile([P, 4 * D], F32, name="junk")
         pst = statp.tile([P, D], F32, name="pst")
@@ -151,9 +152,13 @@ def tile_updateonrightwithselectiveresetonleft_kernel(tc, A1_atop_B1, A2_atop_B2
         def row_max(b, step):
             if b >= B:
                 return
-            if step == 0:
+            if step <= 0:
                 sc[b] = smallp.tile([P, 12], F32, name="sc")
                 kept[b] = smallp.tile([P, 16], F32, name="kept")
+            if step < 0:
+                nc.vector.tensor_scalar(out=hit[b][:], in0=wt[b][:], scalar1=1.0, scalar2=None, op0=ALU.mult,
+                                        op1=ALU.max, accum_out=sc[b][:, 11:12])
+                return
             src = wt[b] if step == 0 else hit[b]
             lo = (0, 0, 2 * D, 3 * D)[step]
             width = 2 * D >> step
@@ -167,11 +172,11 @@ def tile_updateonrightwithselectiveresetonleft_kernel(tc, A1_atop_B1, A2_atop_B2
         def column_sums(b, i, pairs):
             if b >= B:
                 return
-            lo = 32 * b + 2 * i
+            lo = P * b + SUM_COLS * i
             last = (len(pairs) - 1, 15)
             for k, (x, w) in enumerate(pairs):
                 for c in range(16):
-                    nc.tensor.matmul(out=pst[:, lo:lo + 2], lhsT=x[b][:, c * P:(c + 1) * P], rhs=w[:], start=(k == 0 and c == 0),
+                    nc.tensor.matmul(out=pst[:, lo:lo + SUM_COLS], lhsT=x[b][:, c * P:(c + 1) * P], rhs=w[:], start=(k == 0 and c == 0),
                                      stop=((k, c) == last))
 
         def sums_ab(b):
@@ -206,18 +211,19 @@ def tile_updateonrightwithselectiveresetonleft_kernel(tc, A1_atop_B1, A2_atop_B2
             if b >= B:
                 return
             part[b] = smallp.tile([P, 4], F32, name="part")
-            nc.scalar.copy(out=part[b][:], in_=pst[:, 32 * b:32 * b + 4])
+            sums = pst[:, P * b:P * b + 2 * SUM_COLS].rearrange("p (i c) -> p i c", i=2)
+            nc.scalar.copy(out=part[b][:].rearrange("p (i c) -> p i c", i=2), in_=sums[:, :, 0:2])
 
         def sum_partials(b):
             if b >= B:
                 return
-            nc.tensor.matmul(out=pst[:, 32 * b + 8:32 * b + 12], lhsT=ones[:], rhs=part[b][:], start=True, stop=True)
+            nc.tensor.matmul(out=pst[:, P * b + 96:P * b + 100], lhsT=ones[:], rhs=part[b][:], start=True, stop=True)
 
         def totals(b):
             if b >= B:
                 return
             total[b] = smallp.tile([P, 4], F32, name="total")
-            nc.scalar.copy(out=total[b][:], in_=pst[:, 32 * b + 8:32 * b + 12])
+            nc.scalar.copy(out=total[b][:], in_=pst[:, P * b + 96:P * b + 100])
 
         def decide(b, step):
             if b >= B:
@@ -241,7 +247,7 @@ def tile_updateonrightwithselectiveresetonleft_kernel(tc, A1_atop_B1, A2_atop_B2
         def warm(k):
             for i in range(k):
                 acc = bankp.tile([P, D], F32, name="bank")
-                nc.tensor.matmul(out=acc[:], lhsT=fill[:, 0:P], rhs=fill[:], start=True, stop=True)
+                nc.tensor.matmul(out=acc[:, 0:P], lhsT=fill[:], rhs=fill[:], start=True, stop=True)
 
         def dot(b, i=0, parts=1):
             if i == 0:
@@ -310,27 +316,24 @@ def tile_updateonrightwithselectiveresetonleft_kernel(tc, A1_atop_B1, A2_atop_B2
         abs_a1(0)
         turn("a", 0, 0, 0, 0)
         turn("a", 0, 0, 0, 1)
-        row_max(0, 0)
-        row_max(0, 1)
+        row_max(0, -1)
+        warm(2)
+        spread_max(0)
         abs_a1(1)
-        row_max(0, 2)
-        warm(2)
+        whole_max(0)
         quantise("a", 0, 0)
-        row_max(0, 3)
-        warm(2)
+        hits(0)
+        row_max(1, 0)
         turn("a", 0, 1, 0, 0)
         turn("a", 0, 1, 0, 1)
-        row_max(1, 0)
-        spread_max(0)
+        warm(2)
         nonzero_b1(0)
-        whole_max(0)
         row_max(1, 1)
-        hits(0)
+        sums_ab(0)
+        quantise("a", 0, 1)
         row_max(1, 2)
         turn("g", 0, 0, 0, 0)
         turn("g", 0, 0, 0, 1)
-        sums_ab(0)
-        quantise("a", 0, 1)
         sum_hits(0)
         partials(0)
         signed_hits(0)
@@ -338,49 +341,101 @@ def tile_updateonrightwithselectiveresetonleft_kernel(tc, A1_atop_B1, A2_atop_B2
         turn("g", 0, 1, 0, 1)
         sum_partials(0)
         totals(0)
+        row_max(1, 3)
         quantise("g", 0, 0, 0)
         decide(0, 0)
         turn("g", 0, 0, 1, 0)
         turn("g", 0, 0, 1, 1)
         quantise("g", 0, 1, 0)
         decide(0, 1)
-        turn("g", 0, 1, 1, 0)
+        spread_max(1)
+        whole_max(1)
         decide(0, 2)
-        quantise("g", 0, 0, 1)
+        hits(1)
         decide(0, 3)
         decide(0, 4)
+        turn("g", 0, 1, 1, 0)
         turn("g", 0, 1, 1, 1)
-        row_max(1, 3)
+        nonzero_b1(1)
+        quantise("g", 0, 0, 1)
 
-        for b in range(B - 2):
+        b, e, f = 0, 1, 2
+        multiply(b, 0, 0)
+        multiply(b, 0, 1)
+        quantise("g", b, 1, 1)
+        sums_ab(e)
+        sum_hits(e)
+        partials(e)
+        signed_hits(e)
+        load_b1(3)
+        load_a2(3, 0)
+        load_a2(3, 1)
+        for h in range(2):
+            for n in range(N):
+                load_g(3, n, h)
+        alloc_codes(e)
+        turn("a", e, 0, 0, 0)
+        turn("a", e, 0, 0, 1)
+        turn("a", e, 1, 0, 0)
+        quantise("a", e, 0)
+        multiply(b, 0, 2)
+        multiply(b, 0, 3)
+        abs_a1(f)
+        turn("a", e, 1, 0, 1)
+        turn("g", e, 0, 0, 0)
+        sum_partials(e)
+        totals(e)
+        dot(b)
+        turn("g", e, 0, 0, 1)
+        multiply(b, 1, 0)
+        multiply(b, 1, 1)
+        quantise("a", e, 1)
+        decide(e, 0)
+        row_max(f, 0)
+        turn("g", e, 1, 0, 0)
+        turn("g", e, 1, 0, 1)
+        decide(e, 1)
+        quantise("g", e, 0, 0)
+        decide(e, 2)
+        row_max(f, 1)
+        turn("g", e, 0, 1, 0)
+        quantise("g", e, 1, 0)
+        decide(e, 3)
+        decide(e, 4)
+        row_max(f, 2)
+        multiply(b, 1, 2)
+        multiply(b, 1, 3)
+        store(b, 1, 0, 4 * D)
+        coefficient(b)
+        turn("g", e, 0, 1, 1)
+        correct(b, 0, 2)
+        turn("g", e, 1, 1, 0)
+        turn("g", e, 1, 1, 1)
+        quantise("g", e, 0, 1)
+        row_max(f, 3)
+
+        for b in range(1, B - 2):
             e, f = b + 1, b + 2
             multiply(b, 0, 0)
             multiply(b, 0, 1)
             quantise("g", b, 1, 1)
             correct(b - 1, 1, 2)
             nonzero_b1(e)
-            if b == 0:
-                load_b1(3)
-                load_a2(3, 0)
-                load_a2(3, 1)
-                for h in range(2):
-                    for n in range(N):
-                        load_g(3, n, h)
             alloc_codes(e)
             turn("a", e, 0, 0, 0)
             turn("a", e, 0, 0, 1)
             turn("a", e, 1, 0, 0)
-            abs_a1(f)
             quantise("a", e, 0)
             multiply(b, 0, 2)
             multiply(b, 0, 3)
             spread_max(e)
             whole_max(e)
-            row_max(f, 0)
+            abs_a1(f)
             turn("a", e, 1, 0, 1)
             turn("g", e, 0, 0, 0)
             hits(e)
             dot(b)
+            row_max(f, 0)
             turn("g", e, 0, 0, 1)
             multiply(b, 1, 0)
             multiply(b, 1, 1)

@@ -70,11 +70,10 @@ def tile_updateonrightwithselectiveresetonleft_kernel(tc, A1_atop_B1, A2_atop_B2
 
         def load_a2(b, n, halves=1):
             a2[b, n] = a2p.tile([P, 4 * D], BF16, name="a2")
-            dst = a2[b, n][:].rearrange("p (h c) -> p h c", h=2)
-            src = A2_atop_B2[b, n, 0:D, :].rearrange("(h p t) j -> p h (t j)", h=2, p=P, t=2)
+            src = A2_atop_B2[b, n, 0:D, :].rearrange("(p t) j -> p (t j)", p=P, t=4)
             for i in range(halves):
-                hs = slice(i * 2 // halves, (i + 1) * 2 // halves)
-                nc.sync.dma_start(out=dst[:, hs, :], in_=src[:, hs, :])
+                cols = slice(i * 4 * D // halves, (i + 1) * 4 * D // halves)
+                nc.sync.dma_start(out=a2[b, n][:, cols], in_=src[:, cols])
 
         def load_g(b, n, h):
             g[b, n, h] = gp.tile([P, 4 * D], BF16, name="g")
@@ -102,10 +101,12 @@ def tile_updateonrightwithselectiveresetonleft_kernel(tc, A1_atop_B1, A2_atop_B2
             for s in range(4):
                 lo = i * 512 + s * P
                 nc.tensor.transpose(xt[:, s, :], src[:, lo:lo + P], ident[:])
-            half = grp[kind, b, n, h][:].bitcast(F32)[:, i * 512:(i + 1) * 512]
+            words = grp[kind, b, n, h][:].bitcast(F32)
             if kind == "a":
-                nc.scalar.copy(out=half.rearrange("q (r s) -> q r s", s=4), in_=xt.rearrange("q s r -> q r s"))
+                nc.scalar.copy(out=words.rearrange("q (r w) -> q r w", w=8)[:, :, 4 * i:4 * i + 4],
+                               in_=xt.rearrange("q s r -> q r s"))
             else:
+                half = words[:, i * 512:(i + 1) * 512]
                 nc.scalar.copy(out=half.rearrange("q (t r u) -> q t r u", t=2, u=2),
                                in_=xt.rearrange("q (t u) r -> q t r u", t=2, u=2))
 
@@ -261,7 +262,7 @@ def tile_updateonrightwithselectiveresetonleft_kernel(tc, A1_atop_B1, A2_atop_B2
                 nc.tensor.matmul(out=cst[:, b:b + 1], lhsT=kept[b][:, 8:9].to_broadcast([P, P]), rhs=dots[b][:, i:i + 1],
                                  start=(i == 0), stop=(i == parts - 1))
 
-        def correct(b, i, parts):
+        def correct(b, i, parts, stored=True):
             if b < 0:
                 return
             lo, hi = i * 4 * D // parts, (i + 1) * 4 * D // parts
@@ -269,7 +270,8 @@ def tile_updateonrightwithselectiveresetonleft_kernel(tc, A1_atop_B1, A2_atop_B2
             nc.vector.scalar_tensor_tensor(out=osb[b, 0][:, cols], in0=wt[b][:, cols],
                                            scalar=cst[:, b:b + 1], in1=osb[b, 0][:, cols],
                                            op0=ALU.mult, op1=ALU.add)
-            store(b, 0, lo, hi)
+            if stored:
+                store(b, 0, lo, hi)
 
         def store(b, h, lo, hi):
             nc.sync.dma_start(out=out[b, 0, h * D:(h + 1) * D, :].rearrange("(p t) k -> p (t k)", p=P, t=4)[:, lo:hi],
@@ -295,15 +297,15 @@ def tile_updateonrightwithselectiveresetonleft_kernel(tc, A1_atop_B1, A2_atop_B2
         load_g(0, 1, 0)
         load_g(0, 0, 1)
         load_g(0, 1, 1)
-        load_b1(1)
         load_a2(1, 0)
-        load_a2(1, 1)
         load_a1(2)
+        load_b1(1)
+        load_a2(1, 1)
         load_g(1, 0, 0)
         load_g(1, 1, 0)
-        load_b1(2)
         load_g(1, 0, 1)
         load_g(1, 1, 1)
+        load_b1(2)
         load_a2(2, 0)
         load_a2(2, 1)
         load_a1(3)
@@ -329,20 +331,20 @@ def tile_updateonrightwithselectiveresetonleft_kernel(tc, A1_atop_B1, A2_atop_B2
         warm(2)
         nonzero_b1(0)
         row_max(1, 1)
-        sums_ab(0)
         quantise("a", 0, 1)
         row_max(1, 2)
         turn("g", 0, 0, 0, 0)
         turn("g", 0, 0, 0, 1)
+        sums_ab(0)
         sum_hits(0)
         partials(0)
-        signed_hits(0)
         turn("g", 0, 1, 0, 0)
         turn("g", 0, 1, 0, 1)
         sum_partials(0)
         totals(0)
         row_max(1, 3)
         quantise("g", 0, 0, 0)
+        signed_hits(0)
         decide(0, 0)
         turn("g", 0, 0, 1, 0)
         turn("g", 0, 0, 1, 1)
@@ -356,17 +358,15 @@ def tile_updateonrightwithselectiveresetonleft_kernel(tc, A1_atop_B1, A2_atop_B2
         decide(0, 4)
         turn("g", 0, 1, 1, 0)
         turn("g", 0, 1, 1, 1)
-        nonzero_b1(1)
         quantise("g", 0, 0, 1)
 
         b, e, f = 0, 1, 2
         multiply(b, 0, 0)
         multiply(b, 0, 1)
         quantise("g", b, 1, 1)
-        sums_ab(e)
-        sum_hits(e)
-        partials(e)
-        signed_hits(e)
+        abs_a1(f)
+        nonzero_b1(e)
+        row_max(f, 0)
         load_b1(3)
         load_a2(3, 0)
         load_a2(3, 1)
@@ -376,33 +376,35 @@ def tile_updateonrightwithselectiveresetonleft_kernel(tc, A1_atop_B1, A2_atop_B2
         alloc_codes(e)
         turn("a", e, 0, 0, 0)
         turn("a", e, 0, 0, 1)
-        turn("a", e, 1, 0, 0)
         quantise("a", e, 0)
         multiply(b, 0, 2)
         multiply(b, 0, 3)
-        abs_a1(f)
+        sums_ab(e)
+        sum_hits(e)
+        partials(e)
+        signed_hits(e)
+        turn("a", e, 1, 0, 0)
         turn("a", e, 1, 0, 1)
+        dot(b)
         turn("g", e, 0, 0, 0)
         sum_partials(e)
         totals(e)
-        dot(b)
         turn("g", e, 0, 0, 1)
         multiply(b, 1, 0)
         multiply(b, 1, 1)
         quantise("a", e, 1)
         decide(e, 0)
-        row_max(f, 0)
         turn("g", e, 1, 0, 0)
         turn("g", e, 1, 0, 1)
+        row_max(f, 1)
         decide(e, 1)
         quantise("g", e, 0, 0)
         decide(e, 2)
-        row_max(f, 1)
+        row_max(f, 2)
         turn("g", e, 0, 1, 0)
         quantise("g", e, 1, 0)
         decide(e, 3)
         decide(e, 4)
-        row_max(f, 2)
         multiply(b, 1, 2)
         multiply(b, 1, 3)
         store(b, 1, 0, 4 * D)
@@ -495,24 +497,24 @@ def tile_updateonrightwithselectiveresetonleft_kernel(tc, A1_atop_B1, A2_atop_B2
         sum_hits(e)
         partials(e)
         quantise("a", e, 1)
+        turn("g", e, 1, 0, 0)
+        turn("g", e, 1, 0, 1)
         signed_hits(e)
         sum_partials(e)
         totals(e)
-        decide(e, 0)
-        turn("g", e, 1, 0, 0)
-        turn("g", e, 1, 0, 1)
         quantise("g", e, 0, 0)
-        decide(e, 1)
+        decide(e, 0)
         quantise("g", e, 1, 0)
-        decide(e, 2)
+        decide(e, 1)
         multiply(b, 1, 2)
         multiply(b, 1, 3)
         store(b, 1, 0, 4 * D)
         turn("g", e, 0, 1, 0)
         coefficient(b)
+        decide(e, 2)
+        turn("g", e, 0, 1, 1)
         decide(e, 3)
         decide(e, 4)
-        turn("g", e, 0, 1, 1)
         correct(b, 0, 2)
         multiply(e, 0, 0)
         multiply(e, 0, 1)

@@ -322,10 +322,10 @@ def tile_updateonrightwithselectiveresetonleft_kernel(tc, A1_atop_B1, A2_atop_B2
         warm(2)
         spread_max(0)
         abs_a1(1)
-        whole_max(0)
         quantise("a", 0, 0)
-        hits(0)
+        whole_max(0)
         row_max(1, 0)
+        hits(0)
         turn("a", 0, 1, 0, 0)
         turn("a", 0, 1, 0, 1)
         warm(2)
@@ -410,7 +410,7 @@ def tile_updateonrightwithselectiveresetonleft_kernel(tc, A1_atop_B1, A2_atop_B2
         store(b, 1, 0, 4 * D)
         coefficient(b)
         turn("g", e, 0, 1, 1)
-        correct(b, 0, 2)
+        correct(b, 0, 2, stored=False)
         turn("g", e, 1, 1, 0)
         turn("g", e, 1, 1, 1)
         quantise("g", e, 0, 1)
@@ -421,7 +421,8 @@ def tile_updateonrightwithselectiveresetonleft_kernel(tc, A1_atop_B1, A2_atop_B2
             multiply(b, 0, 0)
             multiply(b, 0, 1)
             quantise("g", b, 1, 1)
-            correct(b - 1, 1, 2)
+            correct(b - 1, 1, 2, stored=False)
+            store(b - 1, 0, 0, 4 * D)
             nonzero_b1(e)
             alloc_codes(e)
             turn("a", e, 0, 0, 0)
@@ -465,7 +466,7 @@ def tile_updateonrightwithselectiveresetonleft_kernel(tc, A1_atop_B1, A2_atop_B2
             store(b, 1, 0, 4 * D)
             coefficient(b)
             turn("g", e, 0, 1, 1)
-            correct(b, 0, 2)
+            correct(b, 0, 2, stored=False)
             turn("g", e, 1, 1, 0)
             turn("g", e, 1, 1, 1)
             quantise("g", e, 0, 1)
@@ -475,8 +476,8 @@ def tile_updateonrightwithselectiveresetonleft_kernel(tc, A1_atop_B1, A2_atop_B2
         multiply(b, 0, 0)
         multiply(b, 0, 1)
         quantise("g", b, 1, 1)
-        correct(b - 1, 1, 2)
-        nonzero_b1(e)
+        correct(b - 1, 1, 2, stored=False)
+        store(b - 1, 0, 0, 4 * D)
         alloc_codes(e)
         turn("a", e, 0, 0, 0)
         turn("a", e, 0, 0, 1)
@@ -486,6 +487,7 @@ def tile_updateonrightwithselectiveresetonleft_kernel(tc, A1_atop_B1, A2_atop_B2
         multiply(b, 0, 3)
         spread_max(e)
         whole_max(e)
+        nonzero_b1(e)
         turn("a", e, 1, 0, 1)
         hits(e)
         turn("g", e, 0, 0, 0)

@@ -90,7 +90,7 @@ def tile_updateonrightwithselectiveresetonleft_kernel(tc, A1_atop_B1, A2_atop_B2
                 codep.tile([P, N * D], U8, name="as_", align_bytes=64),
             )
 
-        def turn(kind, b, n, h, i):
+        def turn(kind, b, n, h, i, copy=nc.scalar.copy):
             if b >= B:
                 return
             src = (a2[b, n] if kind == "a" else g[b, n, h])[:].bitcast(F32)
@@ -103,11 +103,11 @@ def tile_updateonrightwithselectiveresetonleft_kernel(tc, A1_atop_B1, A2_atop_B2
                 nc.tensor.transpose(xt[:, s, :], src[:, lo:lo + P], ident[:])
             words = grp[kind, b, n, h][:].bitcast(F32)
             if kind == "a":
-                nc.scalar.copy(out=words.rearrange("q (r w) -> q r w", w=8)[:, :, 4 * i:4 * i + 4],
+                copy(out=words.rearrange("q (r w) -> q r w", w=8)[:, :, 4 * i:4 * i + 4],
                                in_=xt.rearrange("q s r -> q r s"))
             else:
                 half = words[:, i * 512:(i + 1) * 512]
-                nc.scalar.copy(out=half.rearrange("q (t r u) -> q t r u", t=2, u=2),
+                copy(out=half.rearrange("q (t r u) -> q t r u", t=2, u=2),
                                in_=xt.rearrange("q (t u) r -> q t r u", t=2, u=2))
 
         def quantise(kind, b, n, h=0):
@@ -257,9 +257,12 @@ def tile_updateonrightwithselectiveresetonleft_kernel(tc, A1_atop_B1, A2_atop_B2
             nc.vector.scalar_tensor_tensor(out=junk[:, cols], in0=osb[b, 0][:, cols], scalar=1.0, in1=a1[b][:, cols],
                                            op0=ALU.mult, op1=ALU.mult, accum_out=dots[b][:, i:i + 1])
 
+        def factor(b):
+            return cst[:, b:b + 1] if b < B - 1 else pst[:, 4 * P - 1:4 * P]
+
         def coefficient(b, parts=1):
             for i in range(parts):
-                nc.tensor.matmul(out=cst[:, b:b + 1], lhsT=kept[b][:, 8:9].to_broadcast([P, P]), rhs=dots[b][:, i:i + 1],
+                nc.tensor.matmul(out=factor(b), lhsT=kept[b][:, 8:9].to_broadcast([P, P]), rhs=dots[b][:, i:i + 1],
                                  start=(i == 0), stop=(i == parts - 1))
 
         def correct(b, i, parts, stored=True):
@@ -268,7 +271,7 @@ def tile_updateonrightwithselectiveresetonleft_kernel(tc, A1_atop_B1, A2_atop_B2
             lo, hi = i * 4 * D // parts, (i + 1) * 4 * D // parts
             cols = slice(lo, hi)
             nc.vector.scalar_tensor_tensor(out=osb[b, 0][:, cols], in0=wt[b][:, cols],
-                                           scalar=cst[:, b:b + 1], in1=osb[b, 0][:, cols],
+                                           scalar=factor(b), in1=osb[b, 0][:, cols],
                                            op0=ALU.mult, op1=ALU.add)
             if stored:
                 store(b, 0, lo, hi)
@@ -395,11 +398,11 @@ def tile_updateonrightwithselectiveresetonleft_kernel(tc, A1_atop_B1, A2_atop_B2
         quantise("a", e, 1)
         decide(e, 0)
         turn("g", e, 1, 0, 0)
-        turn("g", e, 1, 0, 1)
         row_max(f, 1)
         decide(e, 1)
         quantise("g", e, 0, 0)
         decide(e, 2)
+        turn("g", e, 1, 0, 1, nc.vector.tensor_copy)
         row_max(f, 2)
         turn("g", e, 0, 1, 0)
         quantise("g", e, 1, 0)
@@ -504,10 +507,10 @@ def tile_updateonrightwithselectiveresetonleft_kernel(tc, A1_atop_B1, A2_atop_B2
         signed_hits(e)
         sum_partials(e)
         totals(e)
-        quantise("g", e, 0, 0)
         decide(e, 0)
-        quantise("g", e, 1, 0)
+        quantise("g", e, 0, 0)
         decide(e, 1)
+        quantise("g", e, 1, 0)
         multiply(b, 1, 2)
         multiply(b, 1, 3)
         store(b, 1, 0, 4 * D)
@@ -518,22 +521,24 @@ def tile_updateonrightwithselectiveresetonleft_kernel(tc, A1_atop_B1, A2_atop_B2
         decide(e, 3)
         decide(e, 4)
         correct(b, 0, 2)
-        multiply(e, 0, 0)
-        multiply(e, 0, 1)
         turn("g", e, 1, 1, 0)
         turn("g", e, 1, 1, 1)
+        multiply(e, 0, 0)
+        multiply(e, 0, 1)
         quantise("g", e, 0, 1)
-        correct(b, 1, 2)
         multiply(e, 0, 2)
         multiply(e, 0, 3)
         quantise("g", e, 1, 1)
+        correct(b, 2, 4)
         dot(e, 0, 2)
         multiply(e, 1, 0)
         store(e, 1, 0, D)
         dot(e, 1, 2)
+        correct(b, 3, 4, stored=False)
         for t in range(1, 4):
             multiply(e, 1, t)
             store(e, 1, t * D, (t + 1) * D)
+        store(b, 0, 3 * D, 4 * D)
         coefficient(e, 2)
         for i in range(4):
             correct(e, i, 4)

@@ -30,8 +30,8 @@ def tile_updateonrightwithselectiveresetonleft_kernel(tc, A1_atop_B1, A2_atop_B2
         const = ctx.enter_context(tc.tile_pool(name="const", bufs=1))
         a1p = ctx.enter_context(tc.tile_pool(name="a1p", bufs=4))
         b1p = ctx.enter_context(tc.tile_pool(name="b1p", bufs=2))
-        a2p = ctx.enter_context(tc.tile_pool(name="a2p", bufs=4))
-        gp = ctx.enter_context(tc.tile_pool(name="gp", bufs=8))
+        a2p = ctx.enter_context(tc.tile_pool(name="a2p", bufs=2))
+        gp = ctx.enter_context(tc.tile_pool(name="gp", bufs=4))
         wtp = ctx.enter_context(tc.tile_pool(name="wtp", bufs=3))
         hitp = ctx.enter_context(tc.tile_pool(name="hitp", bufs=2))
         grpp = ctx.enter_context(tc.tile_pool(name="grpp", bufs=6))
@@ -69,16 +69,27 @@ def tile_updateonrightwithselectiveresetonleft_kernel(tc, A1_atop_B1, A2_atop_B2
             nc.sync.dma_start(out=b1[b][:], in_=A1_atop_B1[b, 0, D:2 * D, :].rearrange("(p t) j -> p (t j)", p=P, t=4))
 
         def load_a2(b, n, halves=1):
-            a2[b, n] = a2p.tile([P, 4 * D], BF16, name="a2")
+            if n == 0:
+                a2[b] = a2p.tile([P, N, 4 * D], BF16, name="a2")
             src = A2_atop_B2[b, n, 0:D, :].rearrange("(p t) j -> p (t j)", p=P, t=4)
             for i in range(halves):
                 cols = slice(i * 4 * D // halves, (i + 1) * 4 * D // halves)
-                nc.sync.dma_start(out=a2[b, n][:, cols], in_=src[:, cols])
+                nc.sync.dma_start(out=a2[b][:, n, cols], in_=src[:, cols])
 
         def load_g(b, n, h):
-            g[b, n, h] = gp.tile([P, 4 * D], BF16, name="g")
-            nc.sync.dma_start(out=g[b, n, h][:],
+            if n == 0:
+                g[b, h] = gp.tile([P, N, 4 * D], BF16, name="g")
+            nc.sync.dma_start(out=g[b, h][:, n, :],
                               in_=grad_out[b, n, h * D:(h + 1) * D, :].rearrange("(p t) j -> p (t j)", p=P, t=4))
+
+        def load_a2_pair(b):
+            a2[b] = a2p.tile([P, N, 4 * D], BF16, name="a2")
+            nc.sync.dma_start(out=a2[b][:], in_=A2_atop_B2[b, :, 0:D, :].rearrange("n (p t) j -> p n (t j)", p=P, t=4))
+
+        def load_g_pair(b, h):
+            g[b, h] = gp.tile([P, N, 4 * D], BF16, name="g")
+            nc.sync.dma_start(out=g[b, h][:],
+                              in_=grad_out[b, :, h * D:(h + 1) * D, :].rearrange("n (p t) j -> p n (t j)", p=P, t=4))
 
         def alloc_codes(b):
             if b >= B:
@@ -93,7 +104,7 @@ def tile_updateonrightwithselectiveresetonleft_kernel(tc, A1_atop_B1, A2_atop_B2
         def turn(kind, b, n, h, i, copy=nc.scalar.copy):
             if b >= B:
                 return
-            src = (a2[b, n] if kind == "a" else g[b, n, h])[:].bitcast(F32)
+            src = (a2[b] if kind == "a" else g[b, h])[:, n, :].bitcast(F32)
             if i == 0:
                 grp[kind, b, n, h] = grpp.tile([P, 4 * D], BF16, name="grp", align_bytes=64)
             bank = bankp.tile([P, D], F32, name="bank")
@@ -309,13 +320,10 @@ def tile_updateonrightwithselectiveresetonleft_kernel(tc, A1_atop_B1, A2_atop_B2
         load_g(1, 0, 1)
         load_g(1, 1, 1)
         load_b1(2)
-        load_a2(2, 0)
-        load_a2(2, 1)
+        load_a2_pair(2)
         load_a1(3)
-        load_g(2, 0, 0)
-        load_g(2, 1, 0)
-        load_g(2, 0, 1)
-        load_g(2, 1, 1)
+        load_g_pair(2, 0)
+        load_g_pair(2, 1)
         alloc_codes(0)
         warm(4)
         abs_a1(0)
@@ -371,11 +379,9 @@ def tile_updateonrightwithselectiveresetonleft_kernel(tc, A1_atop_B1, A2_atop_B2
         nonzero_b1(e)
         row_max(f, 0)
         load_b1(3)
-        load_a2(3, 0)
-        load_a2(3, 1)
-        for h in range(2):
-            for n in range(N):
-                load_g(3, n, h)
+        load_a2_pair(3)
+        load_g_pair(3, 0)
+        load_g_pair(3, 1)
         alloc_codes(e)
         turn("a", e, 0, 0, 0)
         turn("a", e, 0, 0, 1)

@@ -325,12 +325,12 @@ def tile_updateonrightwithselectiveresetonleft_kernel(tc, A1_atop_B1, A2_atop_B2
         load_g_pair(2, 0)
         load_g_pair(2, 1)
         alloc_codes(0)
-        warm(4)
+        warm(5)
         abs_a1(0)
         turn("a", 0, 0, 0, 0)
         turn("a", 0, 0, 0, 1)
         row_max(0, -1)
-        warm(2)
+        warm(3)
         spread_max(0)
         abs_a1(1)
         quantise("a", 0, 0)
@@ -339,7 +339,7 @@ def tile_updateonrightwithselectiveresetonleft_kernel(tc, A1_atop_B1, A2_atop_B2
         hits(0)
         turn("a", 0, 1, 0, 0)
         turn("a", 0, 1, 0, 1)
-        warm(2)
+        warm(3)
         nonzero_b1(0)
         row_max(1, 1)
         quantise("a", 0, 1)
@@ -351,6 +351,7 @@ def tile_updateonrightwithselectiveresetonleft_kernel(tc, A1_atop_B1, A2_atop_B2
         partials(0)
         turn("g", 0, 1, 0, 0)
         turn("g", 0, 1, 0, 1)
+        warm(1)
         sum_partials(0)
         totals(0)
         row_max(1, 3)
@@ -361,6 +362,7 @@ def tile_updateonrightwithselectiveresetonleft_kernel(tc, A1_atop_B1, A2_atop_B2
         turn("g", 0, 0, 1, 1)
         quantise("g", 0, 1, 0)
         decide(0, 1)
+        warm(1)
         spread_max(1)
         whole_max(1)
         decide(0, 2)

@@ -339,7 +339,7 @@ def tile_updateonrightwithselectiveresetonleft_kernel(tc, A1_atop_B1, A2_atop_B2
         hits(0)
         turn("a", 0, 1, 0, 0)
         turn("a", 0, 1, 0, 1)
-        warm(3)
+        warm(5)
         nonzero_b1(0)
         row_max(1, 1)
         quantise("a", 0, 1)
@@ -438,6 +438,7 @@ def tile_updateonrightwithselectiveresetonleft_kernel(tc, A1_atop_B1, A2_atop_B2
             alloc_codes(e)
             turn("a", e, 0, 0, 0)
             turn("a", e, 0, 0, 1)
+            warm(1)
             turn("a", e, 1, 0, 0)
             quantise("a", e, 0)
             multiply(b, 0, 2)
@@ -460,6 +461,7 @@ def tile_updateonrightwithselectiveresetonleft_kernel(tc, A1_atop_B1, A2_atop_B2
             signed_hits(e)
             turn("g", e, 1, 0, 0)
             turn("g", e, 1, 0, 1)
+            warm(1)
             quantise("g", e, 0, 0)
             turn("g", e, 0, 1, 0)
             sum_partials(e)

from contextlib import ExitStack

import concourse.mybir as mybir
from concourse.masks import make_identity

F32 = mybir.dt.float32
BF16 = mybir.dt.bfloat16
I32 = mybir.dt.int32
U32 = mybir.dt.uint32
U8 = mybir.dt.uint8
E4 = mybir.dt.float8_e4m3fn_x4
E5 = mybir.dt.float8_e5m2_x4
ALU = mybir.AluOpType
ACTF = mybir.ActivationFunctionType
AX = mybir.AxisListType

B = 4
N = 2
D = 512
P = 128
FLOPS = 2 * B * (2 * D) * D * (N * D)
SUM_COLS = 32
VETO = -float(2 ** 40)
BYTES = B * (2 * D * D * 2 + N * D * D * 2 + N * 2 * D * D * 2 + 2 * D * D * 4)


def tile_updateonrightwithselectiveresetonleft_kernel(tc, A1_atop_B1, A2_atop_B2, grad_out, out):
    nc = tc.nc
    with ExitStack() as ctx:
        const = ctx.enter_context(tc.tile_pool(name="const", bufs=1))
        a1p = ctx.enter_context(tc.tile_pool(name="a1p", bufs=4))
        b1p = ctx.enter_context(tc.tile_pool(name="b1p", bufs=2))
        a2p = ctx.enter_context(tc.tile_pool(name="a2p", bufs=2))
        gp = ctx.enter_context(tc.tile_pool(name="gp", bufs=4))
        wtp = ctx.enter_context(tc.tile_pool(name="wtp", bufs=3))
        hitp = ctx.enter_context(tc.tile_pool(name="hitp", bufs=2))
        grpp = ctx.enter_context(tc.tile_pool(name="grpp", bufs=6))
        codep = ctx.enter_context(tc.tile_pool(name="codep", bufs=2))
        op = ctx.enter_context(tc.tile_pool(name="op", bufs=8))
        smallp = ctx.enter_context(tc.tile_pool(name="smallp", bufs=3))
        bankp = ctx.enter_context(tc.psum_pool(name="bankp", bufs=6))
        statp = ctx.enter_context(tc.psum_pool(name="statp", bufs=1))
        ctx.enter_context(tc.manual_schedule())

        ident = const.tile([P, P], F32, name="ident")
        make_identity(nc, ident[:])
        ones = const.tile([P, P], F32, name="ones")
        nc.vector.memset(ones[:], 1.0)
        onesb = const.tile([P, SUM_COLS], BF16, name="onesb")
        nc.vector.memset(onesb[:], 1.0)
        veto = const.tile([P, SUM_COLS], BF16, name="veto")
        nc.vector.memset(veto[:], VETO)
        fill = const.tile([P, P], F32, name="fill")
        nc.vector.memset(fill[:], 0.0)
        junk = const.tile([P, 4 * D], F32, name="junk")
        pst = statp.tile([P, D], F32, name="pst")
        cst = statp.tile([P, D], F32, name="cst")

        a1, b1, a2, g = {}, {}, {}, {}
        wt, hit, sc, dots, part, total = {}, {}, {}, {}, {}, {}
        grp, codes, osb, spread, kept = {}, {}, {}, {}, {}

        def load_a1(b):
            a1[b] = a1p.tile([P, 4 * D], BF16, name="a1")
            nc.sync.dma_start(out=a1[b][:], in_=A1_atop_B1[b, 0, 0:D, :].rearrange("(p t) j -> p (t j)", p=P, t=4))

        def load_b1(b):
            b1[b] = b1p.tile([P, 4 * D], BF16, name="b1")
            nc.sync.dma_start(out=b1[b][:], in_=A1_atop_B1[b, 0, D:2 * D, :].rearrange("(p t) j -> p (t j)", p=P, t=4))

        def load_a2(b, n, halves=1):
            if n == 0:
                a2[b] = a2p.tile([P, N, 4 * D], BF16, name="a2")
            src = A2_atop_B2[b, n, 0:D, :].rearrange("(p t) j -> p (t j)", p=P, t=4)
            for i in range(halves):
                cols = slice(i * 4 * D // halves, (i + 1) * 4 * D // halves)
                nc.sync.dma_start(out=a2[b][:, n, cols], in_=src[:, cols])

        def load_g(b, n, h):
            if n == 0:
                g[b, h] = gp.tile([P, N, 4 * D], BF16, name="g")
            nc.sync.dma_start(out=g[b, h][:, n, :],
                              in_=grad_out[b, n, h * D:(h + 1) * D, :].rearrange("(p t) j -> p (t j)", p=P, t=4))

        def load_a2_pair(b):
            a2[b] = a2p.tile([P, N, 4 * D], BF16, name="a2")
            nc.sync.dma_start(out=a2[b][:], in_=A2_atop_B2[b, :, 0:D, :].rearrange("n (p t) j -> p n (t j)", p=P, t=4))

        def load_g_pair(b, h):
            g[b, h] = gp.tile([P, N, 4 * D], BF16, name="g")
            nc.sync.dma_start(out=g[b, h][:],
                              in_=grad_out[b, :, h * D:(h + 1) * D, :].rearrange("n (p t) j -> p n (t j)", p=P, t=4))

        def alloc_codes(b):
            if b >= B:
                return
            codes[b] = (
                codep.tile([P, N * 2 * D], U32, name="gc", align_bytes=64),
                codep.tile([P, N * 2 * D], U8, name="gs", align_bytes=64),
                codep.tile([P, N * D], U32, name="ac", align_bytes=64),
                codep.tile([P, N * D], U8, name="as_", align_bytes=64),
            )

        def turn(kind, b, n, h, i, copy=nc.scalar.copy):
            if b >= B:
                return
            src = (a2[b] if kind == "a" else g[b, h])[:, n, :].bitcast(F32)
            if i == 0:
                grp[kind, b, n, h] = grpp.tile([P, 4 * D], BF16, name="grp", align_bytes=64)
            bank = bankp.tile([P, D], F32, name="bank")
            xt = bank[:].rearrange("p (s r) -> p s r", s=4)
            for s in range(4):
                lo = i * 512 + s * P
                nc.tensor.transpose(xt[:, s, :], src[:, lo:lo + P], ident[:])
            words = grp[kind, b, n, h][:].bitcast(F32)
            if kind == "a":
                copy(out=words.rearrange("q (r w) -> q r w", w=8)[:, :, 4 * i:4 * i + 4],
                               in_=xt.rearrange("q s r -> q r s"))
            else:
                half = words[:, i * 512:(i + 1) * 512]
                copy(out=half.rearrange("q (t r u) -> q t r u", t=2, u=2),
                               in_=xt.rearrange("q (t u) r -> q t r u", t=2, u=2))

        def quantise(kind, b, n, h=0):
            if b >= B:
                return
            gc, gs, ac, as_ = codes[b]
            if kind == "a":
                cols = slice(n * D, (n + 1) * D)
                nc.vector.quantize_mx(out=ac[:, cols].bitcast(E4), scales=as_[:, cols], in_=grp[kind, b, n, h][:])
            else:
                lo = n * 2 * D + h * D
                cols = slice(lo, lo + D)
                nc.vector.quantize_mx(out=gc[:, cols].bitcast(E5), scales=gs[:, cols], in_=grp[kind, b, n, h][:])

        def multiply(b, h, t):
            if b < 0:
                return
            gc, gs, ac, as_ = codes[b]
            if t == 0:
                osb[b, h] = op.tile([P, 4 * D], F32, name="osb")
            scale = sc[b][:, 8:9] if h == 0 else kept[b][:, 0:1]
            acc = bankp.tile([P, D], F32, name="bank")
            for n in range(N):
                lo = n * 2 * D + h * D + t * P
                nc.tensor.matmul_mx(out=acc[:], lhsT=gc[:, lo:lo + P].bitcast(E5), lhsT_scale=gs[:, lo:lo + P],
                                    rhs=ac[:, n * D:(n + 1) * D].bitcast(E4), rhs_scale=as_[:, n * D:(n + 1) * D],
                                    start=(n == 0), stop=(n == N - 1))
            nc.scalar.activation(out=osb[b, h][:, t * D:(t + 1) * D], in_=acc[:], func=ACTF.Copy, scale=scale)

        def abs_a1(b):
            if b >= B:
                return
            wt[b] = wtp.tile([P, 4 * D], BF16, name="wt")
            hit[b] = hitp.tile([P, 4 * D], BF16, name="hit")
            nc.vector.tensor_scalar(out=wt[b][:].bitcast(I32), in0=a1[b][:].bitcast(I32), scalar1=0x7FFF7FFF,
                                    scalar2=None, op0=ALU.bitwise_and)

        def nonzero_b1(b):
            if b >= B:
                return
            nc.vector.tensor_scalar(out=b1[b][:], in0=b1[b][:], scalar1=0.0, scalar2=None, op0=ALU.not_equal)

        def row_max(b, step):
            if b >= B:
                return
            if step <= 0:
                sc[b] = smallp.tile([P, 12], F32, name="sc")
                kept[b] = smallp.tile([P, 16], F32, name="kept")
            if step < 0:
                nc.vector.tensor_scalar(out=hit[b][:], in0=wt[b][:], scalar1=1.0, scalar2=None, op0=ALU.mult,
                                        op1=ALU.max, accum_out=sc[b][:, 11:12])
                return
            src = wt[b] if step == 0 else hit[b]
            lo = (0, 0, 2 * D, 3 * D)[step]
            width = 2 * D >> step
            if step == 3:
                nc.vector.tensor_reduce(out=sc[b][:, 11:12], in_=src[:, lo:lo + 2 * width], axis=AX.X, op=ALU.max)
            else:
                dst = (0, 2 * D, 3 * D)[step]
                nc.vector.tensor_tensor(out=hit[b][:, dst:dst + width], in0=src[:, lo:lo + width],
                                        in1=src[:, lo + width:lo + 2 * width], op=ALU.max)

        def column_sums(b, i, pairs):
            if b >= B:
                return
            lo = P * b + SUM_COLS * i
            last = (len(pairs) - 1, 15)
            for k, (x, w) in enumerate(pairs):
                for c in range(16):
                    nc.tensor.matmul(out=pst[:, lo:lo + SUM_COLS], lhsT=x[b][:, c * P:(c + 1) * P], rhs=w[:], start=(k == 0 and c == 0),
                                     stop=((k, c) == last))

        def sums_ab(b):
            column_sums(b, 0, ((wt, onesb), (b1, veto)))

        def sum_hits(b):
            column_sums(b, 1, ((hit, onesb),))

        def spread_max(b):
            if b >= B:
                return
            spread[b] = bankp.tile([P, D], F32, name="bank")
            nc.tensor.matmul(out=spread[b][:, 0:P], lhsT=sc[b][:, 11:12].to_broadcast([P, P]), rhs=ident[:], start=True,
                             stop=True)

        def whole_max(b):
            if b >= B:
                return
            nc.vector.tensor_reduce(out=sc[b][:, 4:5], in_=spread[b][:, 0:P], axis=AX.X, op=ALU.max)

        def hits(b):
            if b >= B:
                return
            nc.vector.tensor_scalar(out=hit[b][:], in0=wt[b][:], scalar1=sc[b][:, 4:5], scalar2=None, op0=ALU.is_equal)

        def signed_hits(b):
            if b >= B:
                return
            nc.vector.tensor_tensor(out=wt[b][:], in0=hit[b][:], in1=a1[b][:], op=ALU.mult)

        def partials(b):
            if b >= B:
                return
            part[b] = smallp.tile([P, 4], F32, name="part")
            sums = pst[:, P * b:P * b + 2 * SUM_COLS].rearrange("p (i c) -> p i c", i=2)
            nc.scalar.copy(out=part[b][:].rearrange("p (i c) -> p i c", i=2), in_=sums[:, :, 0:2])

        def sum_partials(b):
            if b >= B:
                return
            nc.tensor.matmul(out=pst[:, P * b + 96:P * b + 100], lhsT=ones[:], rhs=part[b][:], start=True, stop=True)

        def totals(b):
            if b >= B:
                return
            total[b] = smallp.tile([P, 4], F32, name="total")
            nc.scalar.copy(out=total[b][:], in_=pst[:, P * b + 96:P * b + 100])

        def decide(b, step):
            if b >= B:
                return
            s, t_, k_ = sc[b], total[b], kept[b]
            if step == 0:
                nc.vector.tensor_scalar(out=s[:, 3:4], in0=t_[:, 0:1], scalar1=float(D * D), scalar2=None, op0=ALU.is_gt)
                nc.gpsimd.tensor_scalar(out=k_[:, 0:1], in0=t_[:, 0:1], scalar1=float(D * D), scalar2=None, op0=ALU.is_le)
            if step == 1:
                nc.vector.tensor_scalar(out=s[:, 6:7], in0=s[:, 3:4], scalar1=s[:, 4:5], scalar2=1.0, op0=ALU.mult,
                                        op1=ALU.max)
            if step == 2:
                nc.vector.tensor_scalar(out=s[:, 7:8], in0=s[:, 6:7], scalar1=s[:, 6:7], scalar2=t_[:, 2:3],
                                        op0=ALU.mult, op1=ALU.mult)
            if step == 3:
                nc.vector.reciprocal(out=s[:, 8:10], in_=s[:, 6:8])
            if step == 4:
                nc.gpsimd.tensor_scalar(out=k_[:, 8:9], in0=s[:, 9:10], scalar1=s[:, 3:4], scalar2=-1.0, op0=ALU.mult,
                                        op1=ALU.mult)

        def warm(k):
            for i in range(k):
                acc = bankp.tile([P, D], F32, name="bank")
                nc.tensor.matmul(out=acc[:, 0:P], lhsT=fill[:], rhs=fill[:], start=True, stop=True)

        def dot(b, i=0, parts=1):
            if i == 0:
                dots[b] = smallp.tile([P, 2], F32, name="dots")
            cols = slice(i * 4 * D // parts, (i + 1) * 4 * D // parts)
            nc.vector.scalar_tensor_tensor(out=junk[:, cols], in0=osb[b, 0][:, cols], scalar=1.0, in1=a1[b][:, cols],
                                           op0=ALU.mult, op1=ALU.mult, accum_out=dots[b][:, i:i + 1])

        def factor(b):
            return cst[:, b:b + 1] if b < B - 1 else pst[:, 4 * P - 1:4 * P]

        def coefficient(b, parts=1):
            for i in range(parts):
                nc.tensor.matmul(out=factor(b), lhsT=kept[b][:, 8:9].to_broadcast([P, P]), rhs=dots[b][:, i:i + 1],
                                 start=(i == 0), stop=(i == parts - 1))

        def correct(b, i, parts, stored=True):
            if b < 0:
                return
            lo, hi = i * 4 * D // parts, (i + 1) * 4 * D // parts
            cols = slice(lo, hi)
            nc.vector.scalar_tensor_tensor(out=osb[b, 0][:, cols], in0=wt[b][:, cols],
                                           scalar=factor(b), in1=osb[b, 0][:, cols],
                                           op0=ALU.mult, op1=ALU.add)
            if stored:
                store(b, 0, lo, hi)

        def store(b, h, lo, hi):
            nc.sync.dma_start(out=out[b, 0, h * D:(h + 1) * D, :].rearrange("(p t) k -> p (t k)", p=P, t=4)[:, lo:hi],
                              in_=osb[b, h][:, lo:hi])

        def load_entry(b):
            if b >= B:
                return
            load_a2(b, 0)
            load_a2(b, 1)
            load_a1(b)
            load_b1(b)
            for h in range(2):
                for n in range(N):
                    load_g(b, n, h)

        load_a1(0)
        load_a2(0, 0, halves=2)
        load_a1(1)
        load_a2(0, 1)
        load_b1(0)
        load_g(0, 0, 0)
        load_g(0, 1, 0)
        load_g(0, 0, 1)
        load_g(0, 1, 1)
        load_a2(1, 0)
        load_a1(2)
        load_b1(1)
        load_a2(1, 1)
        load_g(1, 0, 0)
        load_g(1, 1, 0)
        load_g(1, 0, 1)
        load_g(1, 1, 1)
        load_b1(2)
        load_a2_pair(2)
        load_a1(3)
        load_g_pair(2, 0)
        load_g_pair(2, 1)
        alloc_codes(0)
        warm(5)
        abs_a1(0)
        turn("a", 0, 0, 0, 0)
        turn("a", 0, 0, 0, 1)
        row_max(0, -1)
        warm(3)
        spread_max(0)
        abs_a1(1)
        quantise("a", 0, 0)
        whole_max(0)
        row_max(1, 0)
        hits(0)
        turn("a", 0, 1, 0, 0)
        turn("a", 0, 1, 0, 1)
        warm(5)
        nonzero_b1(0)
        row_max(1, 1)
        quantise("a", 0, 1)
        row_max(1, 2)
        turn("g", 0, 0, 0, 0)
        turn("g", 0, 0, 0, 1)
        sums_ab(0)
        sum_hits(0)
        partials(0)
        turn("g", 0, 1, 0, 0)
        turn("g", 0, 1, 0, 1)
        warm(1)
        sum_partials(0)
        totals(0)
        row_max(1, 3)
        quantise("g", 0, 0, 0)
        signed_hits(0)
        decide(0, 0)
        turn("g", 0, 0, 1, 0)
        turn("g", 0, 0, 1, 1)
        quantise("g", 0, 1, 0)
        decide(0, 1)
        warm(1)
        spread_max(1)
        whole_max(1)
        decide(0, 2)
        hits(1)
        decide(0, 3)
        decide(0, 4)
        turn("g", 0, 1, 1, 0)
        turn("g", 0, 1, 1, 1)
        quantise("g", 0, 0, 1)

        b, e, f = 0, 1, 2
        multiply(b, 0, 0)
        multiply(b, 0, 1)
        quantise("g", b, 1, 1)
        abs_a1(f)
        nonzero_b1(e)
        row_max(f, 0)
        load_b1(3)
        load_a2_pair(3)
        load_g_pair(3, 0)
        load_g_pair(3, 1)
        alloc_codes(e)
        turn("a", e, 0, 0, 0)
        turn("a", e, 0, 0, 1)
        quantise("a", e, 0)
        multiply(b, 0, 2)
        multiply(b, 0, 3)
        sums_ab(e)
        sum_hits(e)
        partials(e)
        signed_hits(e)
        turn("a", e, 1, 0, 0)
        turn("a", e, 1, 0, 1)
        dot(b)
        turn("g", e, 0, 0, 0)
        sum_partials(e)
        totals(e)
        turn("g", e, 0, 0, 1)
        multiply(b, 1, 0)
        multiply(b, 1, 1)
        quantise("a", e, 1)
        decide(e, 0)
        turn("g", e, 1, 0, 0)
        row_max(f, 1)
        decide(e, 1)
        quantise("g", e, 0, 0)
        decide(e, 2)
        turn("g", e, 1, 0, 1, nc.vector.tensor_copy)
        row_max(f, 2)
        turn("g", e, 0, 1, 0)
        quantise("g", e, 1, 0)
        decide(e, 3)
        decide(e, 4)
        multiply(b, 1, 2)
        multiply(b, 1, 3)
        store(b, 1, 0, 4 * D)
        coefficient(b)
        turn("g", e, 0, 1, 1)
        correct(b, 0, 2, stored=False)
        turn("g", e, 1, 1, 0)
        turn("g", e, 1, 1, 1)
        quantise("g", e, 0, 1)
        row_max(f, 3)

        for b in range(1, B - 2):
            e, f = b + 1, b + 2
            multiply(b, 0, 0)
            multiply(b, 0, 1)
            quantise("g", b, 1, 1)
            correct(b - 1, 1, 2, stored=False)
            store(b - 1, 0, 0, 4 * D)
            nonzero_b1(e)
            alloc_codes(e)
            turn("a", e, 0, 0, 0)
            turn("a", e, 0, 0, 1)
            warm(1)
            turn("a", e, 1, 0, 0)
            quantise("a", e, 0)
            multiply(b, 0, 2)
            multiply(b, 0, 3)
            spread_max(e)
            whole_max(e)
            abs_a1(f)
            turn("a", e, 1, 0, 1)
            turn("g", e, 0, 0, 0)
            hits(e)
            dot(b)
            row_max(f, 0)
            turn("g", e, 0, 0, 1)
            multiply(b, 1, 0)
            multiply(b, 1, 1)
            sums_ab(e)
            sum_hits(e)
            partials(e)
            quantise("a", e, 1)
            signed_hits(e)
            turn("g", e, 1, 0, 0)
            turn("g", e, 1, 0, 1)
            warm(1)
            quantise("g", e, 0, 0)
            turn("g", e, 0, 1, 0)
            sum_partials(e)
            totals(e)
            decide(e, 0)
            row_max(f, 1)
            decide(e, 1)
            quantise("g", e, 1, 0)
            decide(e, 2)
            row_max(f, 2)
            decide(e, 3)
            decide(e, 4)
            multiply(b, 1, 2)
            multiply(b, 1, 3)
            store(b, 1, 0, 4 * D)
            coefficient(b)
            turn("g", e, 0, 1, 1)
            correct(b, 0, 2, stored=False)
            turn("g", e, 1, 1, 0)
            turn("g", e, 1, 1, 1)
            quantise("g", e, 0, 1)
            row_max(f, 3)

        b, e = B - 2, B - 1
        multiply(b, 0, 0)
        multiply(b, 0, 1)
        quantise("g", b, 1, 1)
        correct(b - 1, 1, 2, stored=False)
        store(b - 1, 0, 0, 4 * D)
        alloc_codes(e)
        turn("a", e, 0, 0, 0)
        turn("a", e, 0, 0, 1)
        turn("a", e, 1, 0, 0)
        quantise("a", e, 0)
        multiply(b, 0, 2)
        multiply(b, 0, 3)
        spread_max(e)
        whole_max(e)
        nonzero_b1(e)
        turn("a", e, 1, 0, 1)
        hits(e)
        turn("g", e, 0, 0, 0)
        turn("g", e, 0, 0, 1)
        dot(b)
        multiply(b, 1, 0)
        multiply(b, 1, 1)
        sums_ab(e)
        sum_hits(e)
        partials(e)
        quantise("a", e, 1)
        turn("g", e, 1, 0, 0)
        turn("g", e, 1, 0, 1)
        signed_hits(e)
        sum_partials(e)
        totals(e)
        decide(e, 0)
        quantise("g", e, 0, 0)
        decide(e, 1)
        quantise("g", e, 1, 0)
        multiply(b, 1, 2)
        multiply(b, 1, 3)
        store(b, 1, 0, 4 * D)
        turn("g", e, 0, 1, 0)
        coefficient(b)
        decide(e, 2)
        turn("g", e, 0, 1, 1)
        decide(e, 3)
        decide(e, 4)
        correct(b, 0, 2)
        turn("g", e, 1, 1, 0)
        turn("g", e, 1, 1, 1)
        multiply(e, 0, 0)
        multiply(e, 0, 1)
        quantise("g", e, 0, 1)
        multiply(e, 0, 2)
        multiply(e, 0, 3)
        quantise("g", e, 1, 1)
        correct(b, 2, 4)
        dot(e, 0, 2)
        multiply(e, 1, 0)
        store(e, 1, 0, D)
        dot(e, 1, 2)
        correct(b, 3, 4, stored=False)
        for t in range(1, 4):
            multiply(e, 1, t)
            store(e, 1, t * D, (t + 1) * D)
        store(b, 0, 3 * D, 4 * D)
        coefficient(e, 2)
        for i in range(4):
            correct(e, i, 4)
